import numpy as np
import ml_dtypes


def mxq(x, axis, fmt="e4m3"):
    dtype, down = {"e4m3": (ml_dtypes.float8_e4m3fn, 7), "e5m2": (ml_dtypes.float8_e5m2, 14)}[fmt]
    v = np.moveaxis(np.asarray(x, np.float32).astype(ml_dtypes.bfloat16).astype(np.float64), axis, -1)
    blocks = v.reshape(v.shape[:-1] + (-1, 32))
    amax = np.abs(blocks).max(-1, keepdims=True)
    byte = np.maximum(np.where(amax > 0, np.frexp(amax)[1] - 1 + 127, 0) - down, 1)
    scale = np.exp2(byte - 127.0)
    codes = (blocks / scale).astype(np.float32).astype(dtype).astype(np.float64)
    return np.moveaxis((codes * scale).reshape(v.shape), -1, axis)


WIDE = False


def mx_kscale(k):
    if not WIDE:
        return np.ones(k)
    levels = np.array([10, -10, 5, -5, 0])
    a = np.random.permutation(np.resize(levels, k // 512 * 4)).reshape(k // 512, 4)
    idx = np.arange(k)
    return np.exp2(a[idx // 512, idx % 128 // 32])


BF16 = ml_dtypes.bfloat16


def bf(x):
    return np.asarray(x, np.float32).astype(BF16)


def f64(x):
    return np.asarray(x).astype(np.float64)


B, HG, H, D, LSEQ, LK, BANK = 1, 48, 8, 128, 1536, 384, 128
N = HG * HG
C = H * D
DILATIONS = (1, 2, 3)
POOL = 2


def setup_inputs():
    s = mx_kscale(C)
    return {"x": bf(np.random.standard_normal((B, N, C)) * s),
            "W_kv": bf(np.random.standard_normal((C, 2 * C)) * 1.6 / np.sqrt(C) / s[:, None]),
            "b_kv": bf(np.random.standard_normal(2 * C) * 0.2),
            "E_k": bf(np.random.standard_normal((LSEQ, LK)) / np.sqrt(LSEQ)),
            "E_v": bf(np.random.standard_normal((LSEQ, LK)) / np.sqrt(LSEQ))}


def reference(x, W_kv, b_kv, E_k, E_v):
    xg = f64(x).reshape(B, HG, HG, C)
    x_multi = np.concatenate([xg[:, ::d, ::d, :].reshape(B, -1, C) for d in DILATIONS], axis=1)
    nm2 = (x_multi.shape[1] // POOL) * POOL
    x_pooled = x_multi[:, :nm2].reshape(B, nm2 // POOL, POOL, C).mean(axis=2)
    xl = x_pooled[:, :LSEQ]
    kv = (mxq(xl, 2, "e4m3") @ mxq(f64(W_kv), 0, "e4m3")) + f64(b_kv)
    k = kv[:, :, :C].reshape(B, LSEQ, H, D).transpose(0, 2, 1, 3)
    v = kv[:, :, C:].reshape(B, LSEQ, H, D).transpose(0, 2, 1, 3)
    k_comp = mxq(f64(E_k), 0, "e4m3").T @ mxq(k, 2, "e4m3")
    v_comp = mxq(f64(E_v), 0, "e4m3").T @ mxq(v, 2, "e4m3")
    return k_comp, v_comp

@@ -1,0 +1,232 @@
+from contextlib import ExitStack
+
+import concourse.mybir as mybir
+from concourse.masks import make_identity
+
+BF16 = mybir.dt.bfloat16
+F32 = mybir.dt.float32
+U32 = mybir.dt.uint32
+U8 = mybir.dt.uint8
+FP8X4 = mybir.dt.float8_e4m3fn_x4
+ADD = mybir.AluOpType.add
+
+P = 128
+PACK = 4
+K_PASS = P * PACK
+
+CHANNELS = 1024
+KV = 2048
+LANDMARKS = 1536
+COMPRESSED = 384
+HEAD = 128
+
+CH_PASSES = CHANNELS // K_PASS
+LM_PASSES = LANDMARKS // K_PASS
+RANGE = 512
+RANGES = KV // RANGE
+HALF = P // 2
+MAIN_TILES = 9
+
+FLOPS = 2 * LANDMARKS * CHANNELS * KV + 2 * 2 * COMPRESSED * LANDMARKS * CHANNELS
+
+
+def regroup(copy, grouped, rows):
+    copy(
+        out=grouped.rearrange("p (c i) t -> p c t i", i=4),
+        in_=rows.rearrange("p t (c i) -> p c t i", i=4),
+    )
+
+
+def quantise(nc, codes, scales, grouped):
+    nc.vector.quantize_mx(
+        out=codes.bitcast(FP8X4),
+        scales=scales,
+        in_=grouped.rearrange("p w t -> p (w t)"),
+    )
+
+
+def tile_efficientmultiscaledilatedattention_pa_kernel(
+    tc, x, W_kv, b_kv, E_k, E_v, out_0, out_1
+):
+    nc = tc.nc
+    with ExitStack() as ctx:
+        keep = ctx.enter_context(tc.tile_pool(name="keep", bufs=1))
+        w_stage = ctx.enter_context(tc.tile_pool(name="w_stage", bufs=3))
+        xl_stage = ctx.enter_context(tc.tile_pool(name="xl_stage", bufs=3))
+        kv_stage = ctx.enter_context(tc.tile_pool(name="kv_stage", bufs=3))
+        kv_keep = ctx.enter_context(tc.tile_pool(name="kv_keep", bufs=2))
+        out_stage = ctx.enter_context(tc.tile_pool(name="out_stage", bufs=4))
+        banks = ctx.enter_context(tc.psum_pool(name="banks", bufs=5))
+        comp_banks = ctx.enter_context(tc.psum_pool(name="comp_banks", bufs=1))
+
+        ident = keep.tile([P, P], BF16)
+        make_identity(nc, ident[:])
+        pairs = ident[:].rearrange("p (j e) -> p j e", e=2)
+        pair_sum = keep.tile([P, HALF], BF16)
+        nc.vector.tensor_tensor(out=pair_sum[:], in0=pairs[:, :, 0], in1=pairs[:, :, 1], op=ADD)
+        pool_mat = keep.tile([P, HALF], BF16)
+        nc.vector.tensor_scalar_mul(out=pool_mat[:], in0=pair_sum[:], scalar1=0.5)
+
+        bias = keep.tile([P, KV], BF16)
+        nc.scalar.dma_start(out=bias[:], in_=b_kv.partition_broadcast(P))
+
+        w_view = W_kv.rearrange("(s p) n -> p s n", p=P)
+        w_raw = keep.tile([P, CH_PASSES * PACK, KV], BF16)
+
+        def load_weights(r):
+            cols = slice(RANGE * r, RANGE * (r + 1))
+            nc.sync.dma_start(out=w_raw[:, :, cols], in_=w_view[:, :, cols])
+
+        load_weights(0)
+
+        tokens = x.flatten_outer_dims()
+        token_tiles = []
+        for m in range(MAIN_TILES):
+            x_main = keep.tile([P, 2, CHANNELS], BF16, name="x_main%d" % m)
+            nc.sync.dma_start(
+                out=x_main[:],
+                in_=tokens[2 * P * m : 2 * P * (m + 1), :].rearrange("(e p) c -> p e c", p=P),
+            )
+            token_tiles.extend([x_main[:, 0, :], x_main[:, 1, :]])
+
+        x_tail = keep.tile([P, 6, CHANNELS], BF16)
+        by_two = tokens.rearrange("(k b r c e) d -> b r e c k d", k=6, b=4, r=2, c=24, e=2)
+        for b in range(4):
+            nc.sync.dma_start(out=x_tail[24 * b : 24 * (b + 1), :, :], in_=by_two[b, 0, 0])
+        by_three = tokens.rearrange("(k b r c e) d -> b r e c k d", k=8, b=2, r=3, c=16, e=3)
+        for b in range(2):
+            nc.sync.dma_start(
+                out=x_tail[96 + 16 * b : 96 + 16 * (b + 1), :, :], in_=by_three[b, 0, 0][:, 0:6, :]
+            )
+        token_tiles.extend([x_tail[:, k, :] for k in range(6)])
+
+        load_weights(1)
+        e_raw = []
+        e_raw_k = keep.tile([P, LM_PASSES * PACK, COMPRESSED], BF16)
+        nc.sync.dma_start(out=e_raw_k[:], in_=E_k.rearrange("(s p) j -> p s j", p=P))
+        load_weights(2)
+        load_weights(3)
+        e_raw_v = keep.tile([P, LM_PASSES * PACK, COMPRESSED], BF16)
+        nc.sync.dma_start(out=e_raw_v[:], in_=E_v.rearrange("(s p) j -> p s j", p=P))
+        e_raw.extend([e_raw_k, e_raw_v])
+
+        w_codes = keep.tile([P, CH_PASSES, KV], U32, align_bytes=64)
+        w_scales = keep.tile([P, CH_PASSES, KV], U8, align_bytes=64)
+        xl_codes = keep.tile([P, CH_PASSES, LANDMARKS], U32, align_bytes=64)
+        xl_scales = keep.tile([P, CH_PASSES, LANDMARKS], U8, align_bytes=64)
+        e_codes = [
+            keep.tile([P, LM_PASSES, COMPRESSED], U32, align_bytes=64, name="e_codes%d" % i)
+            for i in range(2)
+        ]
+        e_scales = [
+            keep.tile([P, LM_PASSES, COMPRESSED], U8, align_bytes=64, name="e_scales%d" % i)
+            for i in range(2)
+        ]
+
+        def prepare_weights(r, copy):
+            cols = slice(RANGE * r, RANGE * (r + 1))
+            for c in range(CH_PASSES):
+                w_grp = w_stage.tile([P, RANGE, PACK], BF16, align_bytes=64)
+                regroup(copy, w_grp[:], w_raw[:, PACK * c : PACK * (c + 1), cols])
+                quantise(nc, w_codes[:, c, cols], w_scales[:, c, cols], w_grp[:])
+
+        def prepare_compressor(i):
+            for g in range(LM_PASSES):
+                e_grp = w_stage.tile([P, COMPRESSED, PACK], BF16, align_bytes=64)
+                regroup(nc.scalar.copy, e_grp[:], e_raw[i][:, PACK * g : PACK * (g + 1), :])
+                for lo, hi in ((0, 256), (256, 384)):
+                    quantise(nc, e_codes[i][:, g, lo:hi], e_scales[i][:, g, lo:hi], e_grp[:, lo:hi, :])
+
+        def landmarks(g):
+            for c in range(CH_PASSES):
+                xl_grp = xl_stage.tile([P, K_PASS, PACK], BF16, align_bytes=64)
+                for t in range(PACK):
+                    m = PACK * g + t
+                    mean = banks.tile([P, PACK, P], F32, tag="bank")
+                    for s in range(PACK):
+                        chans = slice(K_PASS * c + P * s, K_PASS * c + P * (s + 1))
+                        for e in range(2):
+                            nc.tensor.matmul(
+                                out=mean[:, s, HALF * e : HALF * (e + 1)],
+                                lhsT=token_tiles[2 * m + e][:, chans],
+                                rhs=pool_mat[:],
+                                start=True,
+                                stop=True,
+                            )
+                    if m < MAIN_TILES:
+                        nc.scalar.copy(
+                            out=xl_grp[:, P * t : P * (t + 1), :],
+                            in_=mean[:].rearrange("p s l -> p l s"),
+                        )
+                    else:
+                        v = m - MAIN_TILES
+                        halves = mean[:].rearrange("p s (e j) -> p e j s", e=2)
+                        two = P + 96 * v
+                        nc.scalar.copy(
+                            out=xl_grp[:, two : two + 96, :].rearrange("p (e j) s -> p e j s", e=2),
+                            in_=halves[:, :, 0:48, :],
+                        )
+                        three = P + 288 + 32 * v
+                        nc.scalar.copy(
+                            out=xl_grp[:, three : three + 32, :].rearrange("p (e j) s -> p e j s", e=2),
+                            in_=halves[:, :, 48:64, :],
+                        )
+                lms = slice(K_PASS * g, K_PASS * (g + 1))
+                quantise(nc, xl_codes[:, c, lms], xl_scales[:, c, lms], xl_grp[:])
+
+        prepare_weights(0, nc.vector.tensor_copy)
+        for g in range(LM_PASSES):
+            landmarks(g)
+
+        outs = [out_0, out_1]
+        for r in range(RANGES):
+            if r + 1 < RANGES:
+                prepare_weights(r + 1, nc.scalar.copy)
+            if r % 2 == 0:
+                prepare_compressor(r // 2)
+            kv_codes = kv_keep.tile([P, LM_PASSES, RANGE], U32, align_bytes=64)
+            kv_scales = kv_keep.tile([P, LM_PASSES, RANGE], U8, align_bytes=64)
+            comp = [comp_banks.tile([P, RANGE], F32, name="comp%d" % j) for j in range(3)]
+            for g in range(LM_PASSES):
+                kv_grp = kv_stage.tile([P, RANGE, PACK], BF16, align_bytes=64)
+                for ct in range(RANGE // P):
+                    cols = slice(RANGE * r + P * ct, RANGE * r + P * (ct + 1))
+                    acc = banks.tile([P, PACK, P], F32, tag="bank")
+                    for t in range(PACK):
+                        lms = slice(K_PASS * g + P * t, K_PASS * g + P * (t + 1))
+                        for c in range(CH_PASSES):
+                            nc.tensor.matmul_mx(
+                                out=acc[:, t, :],
+                                lhsT=xl_codes[:, c, lms].bitcast(FP8X4),
+                                lhsT_scale=xl_scales[:, c, lms],
+                                rhs=w_codes[:, c, cols].bitcast(FP8X4),
+                                rhs_scale=w_scales[:, c, cols],
+                                start=(c == 0),
+                                stop=(c == CH_PASSES - 1),
+                            )
+                    nc.vector.tensor_tensor(
+                        out=kv_grp[:, P * ct : P * (ct + 1), :],
+                        in0=acc[:].rearrange("p t n -> p n t"),
+                        in1=bias[:, cols].unsqueeze(2).to_broadcast([P, P, PACK]),
+                        op=ADD,
+                    )
+                quantise(nc, kv_codes[:, g, :], kv_scales[:, g, :], kv_grp[:])
+                for j in range(3):
+                    rows = slice(P * j, P * (j + 1))
+                    nc.tensor.matmul_mx(
+                        out=comp[j][:],
+                        lhsT=e_codes[r // 2][:, g, rows].bitcast(FP8X4),
+                        lhsT_scale=e_scales[r // 2][:, g, rows],
+                        rhs=kv_codes[:, g, :].bitcast(FP8X4),
+                        rhs_scale=kv_scales[:, g, :],
+                        start=(g == 0),
+                        stop=(g == LM_PASSES - 1),
+                    )
+            heads = slice(4 * (r % 2), 4 * (r % 2) + 4)
+            for j in range(3):
+                result = out_stage.tile([P, RANGE], F32)
+                nc.scalar.copy(out=result[:], in_=comp[j][:])
+                nc.sync.dma_start(
+                    out=outs[r // 2][0, heads, P * j : P * (j + 1), :].rearrange("h j d -> j h d"),
+                    in_=result[:].rearrange("p (h d) -> p h d", d=HEAD),
+                )

@@ -21,11 +21,15 @@ COMPRESSED = 384
 HEAD = 128
 
 CH_PASSES = CHANNELS // K_PASS
-LM_PASSES = LANDMARKS // K_PASS
+GROUPS = LANDMARKS // K_PASS
 RANGE = 512
 RANGES = KV // RANGE
+BANKS = RANGE // P
+OUT_TILES = COMPRESSED // P
 HALF = P // 2
 MAIN_TILES = 9
+
+UNITS = [(r, g) for g in range(GROUPS) for r in (0, 1)] + [(r, g) for r in (2, 3) for g in range(GROUPS)]
 
 FLOPS = 2 * LANDMARKS * CHANNELS * KV + 2 * 2 * COMPRESSED * LANDMARKS * CHANNELS
 
@@ -50,38 +54,32 @@ def tile_efficientmultiscaledilatedattention_pa_kernel(
 ):
     nc = tc.nc
     with ExitStack() as ctx:
+        ctx.enter_context(tc.manual_schedule())
         keep = ctx.enter_context(tc.tile_pool(name="keep", bufs=1))
-        w_stage = ctx.enter_context(tc.tile_pool(name="w_stage", bufs=3))
-        xl_stage = ctx.enter_context(tc.tile_pool(name="xl_stage", bufs=3))
-        kv_stage = ctx.enter_context(tc.tile_pool(name="kv_stage", bufs=3))
-        kv_keep = ctx.enter_context(tc.tile_pool(name="kv_keep", bufs=2))
+        w_stage = ctx.enter_context(tc.tile_pool(name="w_stage", bufs=4))
+        e_stage = ctx.enter_context(tc.tile_pool(name="e_stage", bufs=3))
+        xl_stage = ctx.enter_context(tc.tile_pool(name="xl_stage", bufs=4))
+        kv_stage = ctx.enter_context(tc.tile_pool(name="kv_stage", bufs=4))
+        kv_keep = ctx.enter_context(tc.tile_pool(name="kv_keep", bufs=3))
         out_stage = ctx.enter_context(tc.tile_pool(name="out_stage", bufs=4))
-        banks = ctx.enter_context(tc.psum_pool(name="banks", bufs=5))
-        comp_banks = ctx.enter_context(tc.psum_pool(name="comp_banks", bufs=1))
+        acc_banks = ctx.enter_context(tc.psum_pool(name="acc_banks", bufs=BANKS))
+        side_banks = ctx.enter_context(tc.psum_pool(name="side_banks", bufs=4))
 
-        ident = keep.tile([P, P], BF16)
-        make_identity(nc, ident[:])
-        pairs = ident[:].rearrange("p (j e) -> p j e", e=2)
-        pair_sum = keep.tile([P, HALF], BF16)
-        nc.vector.tensor_tensor(out=pair_sum[:], in0=pairs[:, :, 0], in1=pairs[:, :, 1], op=ADD)
-        pool_mat = keep.tile([P, HALF], BF16)
-        nc.vector.tensor_scalar_mul(out=pool_mat[:], in0=pair_sum[:], scalar1=0.5)
-
-        bias = keep.tile([P, KV], BF16)
-        nc.scalar.dma_start(out=bias[:], in_=b_kv.partition_broadcast(P))
+        bias_in = keep.tile([1, KV], BF16)
+        nc.sync.dma_start(out=bias_in[:], in_=b_kv.unsqueeze(0))
 
         w_view = W_kv.rearrange("(s p) n -> p s n", p=P)
-        w_raw = keep.tile([P, CH_PASSES * PACK, KV], BF16)
+        w_raw = [
+            keep.tile([P, CH_PASSES * PACK, RANGE], BF16, name="w_raw%d" % r) for r in range(RANGES)
+        ]
 
         def load_weights(r):
-            cols = slice(RANGE * r, RANGE * (r + 1))
-            nc.sync.dma_start(out=w_raw[:, :, cols], in_=w_view[:, :, cols])
-
-        load_weights(0)
+            nc.sync.dma_start(out=w_raw[r][:], in_=w_view[:, :, RANGE * r : RANGE * (r + 1)])
 
         tokens = x.flatten_outer_dims()
         token_tiles = []
-        for m in range(MAIN_TILES):
+
+        def load_main(m):
             x_main = keep.tile([P, 2, CHANNELS], BF16, name="x_main%d" % m)
             nc.sync.dma_start(
                 out=x_main[:],
@@ -89,144 +87,254 @@ def tile_efficientmultiscaledilatedattention_pa_kernel(
             )
             token_tiles.extend([x_main[:, 0, :], x_main[:, 1, :]])
 
+        load_weights(0)
+        for m in range(PACK):
+            load_main(m)
+        load_weights(1)
+        for m in range(PACK, MAIN_TILES):
+            load_main(m)
+
         x_tail = keep.tile([P, 6, CHANNELS], BF16)
         by_two = tokens.rearrange("(k b r c e) d -> b r e c k d", k=6, b=4, r=2, c=24, e=2)
         for b in range(4):
-            nc.sync.dma_start(out=x_tail[24 * b : 24 * (b + 1), :, :], in_=by_two[b, 0, 0])
+            nc.sync.dma_start(out=x_tail[b:96:4, :, :], in_=by_two[b, 0, 0])
         by_three = tokens.rearrange("(k b r c e) d -> b r e c k d", k=8, b=2, r=3, c=16, e=3)
         for b in range(2):
-            nc.sync.dma_start(
-                out=x_tail[96 + 16 * b : 96 + 16 * (b + 1), :, :], in_=by_three[b, 0, 0][:, 0:6, :]
-            )
+            nc.sync.dma_start(out=x_tail[96 + b : P : 2, :, :], in_=by_three[b, 0, 0][:, 0:6, :])
         token_tiles.extend([x_tail[:, k, :] for k in range(6)])
 
-        load_weights(1)
-        e_raw = []
-        e_raw_k = keep.tile([P, LM_PASSES * PACK, COMPRESSED], BF16)
-        nc.sync.dma_start(out=e_raw_k[:], in_=E_k.rearrange("(s p) j -> p s j", p=P))
+        e_raw = [
+            keep.tile([P, GROUPS * PACK, COMPRESSED], BF16, name="e_raw%d" % h) for h in range(2)
+        ]
         load_weights(2)
+        nc.sync.dma_start(out=e_raw[0][:], in_=E_k.rearrange("(s p) j -> p s j", p=P))
         load_weights(3)
-        e_raw_v = keep.tile([P, LM_PASSES * PACK, COMPRESSED], BF16)
-        nc.sync.dma_start(out=e_raw_v[:], in_=E_v.rearrange("(s p) j -> p s j", p=P))
-        e_raw.extend([e_raw_k, e_raw_v])
+        nc.sync.dma_start(out=e_raw[1][:], in_=E_v.rearrange("(s p) j -> p s j", p=P))
+
+        ident = keep.tile([P, P], BF16)
+        make_identity(nc, ident[:])
+        half_ident = keep.tile([P, P], BF16)
+        nc.vector.tensor_scalar_mul(out=half_ident[:], in0=ident[:], scalar1=0.5)
+        main_mat = keep.tile([P, HALF], BF16)
+        pairs = half_ident[:].rearrange("p (j e) -> p j e", e=2)
+        nc.vector.tensor_tensor(out=main_mat[:], in0=pairs[:, :, 0], in1=pairs[:, :, 1], op=ADD)
+        tail_mat = keep.tile([P, HALF], BF16)
+        two = half_ident[:, 0:96].rearrange("p (u e b) -> p b u e", u=12, e=2, b=4)
+        nc.vector.tensor_tensor(
+            out=tail_mat[:, 0:48].rearrange("p (b u) -> p b u", b=4),
+            in0=two[:, :, :, 0],
+            in1=two[:, :, :, 1],
+            op=ADD,
+        )
+        three = half_ident[:, 96:P].rearrange("p (u e b) -> p b u e", u=8, e=2, b=2)
+        nc.vector.tensor_tensor(
+            out=tail_mat[:, 48:64].rearrange("p (b u) -> p b u", b=2),
+            in0=three[:, :, :, 0],
+            in1=three[:, :, :, 1],
+            op=ADD,
+        )
+
+        ones = keep.tile([P, P], BF16)
+        nc.vector.memset(ones[:], 1.0)
+        bias_row = keep.tile([P, KV], BF16)
+        nc.vector.memset(bias_row[:], 0.0)
+        nc.vector.tensor_copy(out=bias_row[0:1, :], in_=bias_in[:])
+        bias = keep.tile([P, KV], BF16)
+        for r in range(RANGES):
+            cols = slice(RANGE * r, RANGE * (r + 1))
+            spread = side_banks.tile([P, RANGE], F32, tag="side")
+            nc.tensor.matmul(out=spread[:], lhsT=ones[:], rhs=bias_row[:, cols], start=True, stop=True)
+            nc.scalar.copy(out=bias[:, cols], in_=spread[:])
 
         w_codes = keep.tile([P, CH_PASSES, KV], U32, align_bytes=64)
         w_scales = keep.tile([P, CH_PASSES, KV], U8, align_bytes=64)
         xl_codes = keep.tile([P, CH_PASSES, LANDMARKS], U32, align_bytes=64)
         xl_scales = keep.tile([P, CH_PASSES, LANDMARKS], U8, align_bytes=64)
         e_codes = [
-            keep.tile([P, LM_PASSES, COMPRESSED], U32, align_bytes=64, name="e_codes%d" % i)
-            for i in range(2)
+            keep.tile([P, GROUPS, COMPRESSED], U32, align_bytes=64, name="e_codes%d" % h)
+            for h in range(2)
         ]
         e_scales = [
-            keep.tile([P, LM_PASSES, COMPRESSED], U8, align_bytes=64, name="e_scales%d" % i)
-            for i in range(2)
+            keep.tile([P, GROUPS, COMPRESSED], U8, align_bytes=64, name="e_scales%d" % h)
+            for h in range(2)
         ]
 
-        def prepare_weights(r, copy):
-            cols = slice(RANGE * r, RANGE * (r + 1))
+        w_grouped = {}
+
+        def regroup_weights(r, copies):
             for c in range(CH_PASSES):
                 w_grp = w_stage.tile([P, RANGE, PACK], BF16, align_bytes=64)
-                regroup(copy, w_grp[:], w_raw[:, PACK * c : PACK * (c + 1), cols])
-                quantise(nc, w_codes[:, c, cols], w_scales[:, c, cols], w_grp[:])
+                regroup(copies[c], w_grp[:], w_raw[r][:, PACK * c : PACK * (c + 1), :])
+                w_grouped[(r, c)] = w_grp
 
-        def prepare_compressor(i):
-            for g in range(LM_PASSES):
-                e_grp = w_stage.tile([P, COMPRESSED, PACK], BF16, align_bytes=64)
-                regroup(nc.scalar.copy, e_grp[:], e_raw[i][:, PACK * g : PACK * (g + 1), :])
-                for lo, hi in ((0, 256), (256, 384)):
-                    quantise(nc, e_codes[i][:, g, lo:hi], e_scales[i][:, g, lo:hi], e_grp[:, lo:hi, :])
-
-        def landmarks(g):
+        def quantise_weights(r):
+            cols = slice(RANGE * r, RANGE * (r + 1))
             for c in range(CH_PASSES):
-                xl_grp = xl_stage.tile([P, K_PASS, PACK], BF16, align_bytes=64)
-                for t in range(PACK):
-                    m = PACK * g + t
-                    mean = banks.tile([P, PACK, P], F32, tag="bank")
-                    for s in range(PACK):
-                        chans = slice(K_PASS * c + P * s, K_PASS * c + P * (s + 1))
-                        for e in range(2):
-                            nc.tensor.matmul(
-                                out=mean[:, s, HALF * e : HALF * (e + 1)],
-                                lhsT=token_tiles[2 * m + e][:, chans],
-                                rhs=pool_mat[:],
-                                start=True,
-                                stop=True,
-                            )
-                    if m < MAIN_TILES:
-                        nc.scalar.copy(
-                            out=xl_grp[:, P * t : P * (t + 1), :],
-                            in_=mean[:].rearrange("p s l -> p l s"),
-                        )
-                    else:
-                        v = m - MAIN_TILES
-                        halves = mean[:].rearrange("p s (e j) -> p e j s", e=2)
-                        two = P + 96 * v
-                        nc.scalar.copy(
-                            out=xl_grp[:, two : two + 96, :].rearrange("p (e j) s -> p e j s", e=2),
-                            in_=halves[:, :, 0:48, :],
-                        )
-                        three = P + 288 + 32 * v
-                        nc.scalar.copy(
-                            out=xl_grp[:, three : three + 32, :].rearrange("p (e j) s -> p e j s", e=2),
-                            in_=halves[:, :, 48:64, :],
-                        )
-                lms = slice(K_PASS * g, K_PASS * (g + 1))
-                quantise(nc, xl_codes[:, c, lms], xl_scales[:, c, lms], xl_grp[:])
+                quantise(nc, w_codes[:, c, cols], w_scales[:, c, cols], w_grouped[(r, c)][:])
 
-        prepare_weights(0, nc.vector.tensor_copy)
-        for g in range(LM_PASSES):
-            landmarks(g)
+        e_grouped = {}
+
+        def regroup_compressor(h):
+            for g in range(GROUPS):
+                e_grp = e_stage.tile([P, COMPRESSED, PACK], BF16, align_bytes=64)
+                regroup(nc.scalar.copy, e_grp[:], e_raw[h][:, PACK * g : PACK * (g + 1), :])
+                e_grouped[(h, g)] = e_grp
+
+        def quantise_compressor(h):
+            for g in range(GROUPS):
+                for lo, hi in ((0, 256), (256, 384)):
+                    quantise(
+                        nc, e_codes[h][:, g, lo:hi], e_scales[h][:, g, lo:hi], e_grouped[(h, g)][:, lo:hi, :]
+                    )
+
+        xl_grouped = {}
+
+        def pool_landmarks(g, t, copies):
+            m = PACK * g + t
+            for c in range(CH_PASSES):
+                if t == 0:
+                    xl_grouped[(g, c)] = xl_stage.tile(
+                        [P, K_PASS, PACK], BF16, align_bytes=64, name="xl_grp"
+                    )
+                xl_grp = xl_grouped[(g, c)]
+                mean = side_banks.tile([P, PACK, P], F32, tag="side")
+                for s in range(PACK):
+                    chans = slice(K_PASS * c + P * s, K_PASS * c + P * (s + 1))
+                    for e in range(2):
+                        nc.tensor.matmul(
+                            out=mean[:, s, HALF * e : HALF * (e + 1)],
+                            lhsT=token_tiles[2 * m + e][:, chans],
+                            rhs=(main_mat if m < MAIN_TILES else tail_mat)[:],
+                            start=True,
+                            stop=True,
+                        )
+                if m < MAIN_TILES:
+                    copies[c](
+                        out=xl_grp[:, P * t : P * (t + 1), :], in_=mean[:].rearrange("p s l -> p l s")
+                    )
+                else:
+                    v = m - MAIN_TILES
+                    halves = mean[:].rearrange("p s (e j) -> p e j s", e=2)
+                    first = P + 96 * v
+                    copies[c](
+                        out=xl_grp[:, first : first + 96, :].rearrange("p (e j) s -> p e j s", e=2),
+                        in_=halves[:, :, 0:48, :],
+                    )
+                    first = P + 288 + 32 * v
+                    copies[c](
+                        out=xl_grp[:, first : first + 32, :].rearrange("p (e j) s -> p e j s", e=2),
+                        in_=halves[:, :, 48:64, :],
+                    )
+
+        def quantise_landmarks(g):
+            lms = slice(K_PASS * g, K_PASS * (g + 1))
+            for c in range(CH_PASSES):
+                quantise(nc, xl_codes[:, c, lms], xl_scales[:, c, lms], xl_grouped[(g, c)][:])
+
+        acc = {}
+        kv_codes = {}
+        kv_scales = {}
+
+        def multiply(u, ct):
+            r, g = UNITS[u]
+            cols = slice(RANGE * r + P * ct, RANGE * r + P * (ct + 1))
+            bank = acc_banks.tile([P, PACK, P], F32, tag="acc")
+            for t in range(PACK):
+                lms = slice(K_PASS * g + P * t, K_PASS * g + P * (t + 1))
+                for c in range(CH_PASSES):
+                    nc.tensor.matmul_mx(
+                        out=bank[:, t, :],
+                        lhsT=xl_codes[:, c, lms].bitcast(FP8X4),
+                        lhsT_scale=xl_scales[:, c, lms],
+                        rhs=w_codes[:, c, cols].bitcast(FP8X4),
+                        rhs_scale=w_scales[:, c, cols],
+                        start=(c == 0),
+                        stop=(c == CH_PASSES - 1),
+                    )
+            acc[(u, ct)] = bank
+
+        def drain(u, ct):
+            r, g = UNITS[u]
+            if g == 0 and ct == 0:
+                kv_codes[r] = kv_keep.tile([P, GROUPS, RANGE], U32, align_bytes=64, name="kv_codes")
+                kv_scales[r] = kv_keep.tile([P, GROUPS, RANGE], U8, align_bytes=64, name="kv_scales")
+            cols = slice(RANGE * r + P * ct, RANGE * r + P * (ct + 1))
+            kv_grp = kv_stage.tile([P, P, PACK], BF16, align_bytes=64)
+            nc.vector.tensor_tensor(
+                out=kv_grp[:],
+                in0=acc[(u, ct)][:].rearrange("p t n -> p n t"),
+                in1=bias[:, cols].unsqueeze(2).to_broadcast([P, P, PACK]),
+                op=ADD,
+            )
+            return (r, g, ct, kv_grp)
+
+        def quantise_bank(r, g, ct, kv_grp):
+            part = slice(P * ct, P * (ct + 1))
+            quantise(nc, kv_codes[r][:, g, part], kv_scales[r][:, g, part], kv_grp[:])
 
         outs = [out_0, out_1]
-        for r in range(RANGES):
-            if r + 1 < RANGES:
-                prepare_weights(r + 1, nc.scalar.copy)
-            if r % 2 == 0:
-                prepare_compressor(r // 2)
-            kv_codes = kv_keep.tile([P, LM_PASSES, RANGE], U32, align_bytes=64)
-            kv_scales = kv_keep.tile([P, LM_PASSES, RANGE], U8, align_bytes=64)
-            comp = [comp_banks.tile([P, RANGE], F32, name="comp%d" % j) for j in range(3)]
-            for g in range(LM_PASSES):
-                kv_grp = kv_stage.tile([P, RANGE, PACK], BF16, align_bytes=64)
-                for ct in range(RANGE // P):
-                    cols = slice(RANGE * r + P * ct, RANGE * r + P * (ct + 1))
-                    acc = banks.tile([P, PACK, P], F32, tag="bank")
-                    for t in range(PACK):
-                        lms = slice(K_PASS * g + P * t, K_PASS * g + P * (t + 1))
-                        for c in range(CH_PASSES):
-                            nc.tensor.matmul_mx(
-                                out=acc[:, t, :],
-                                lhsT=xl_codes[:, c, lms].bitcast(FP8X4),
-                                lhsT_scale=xl_scales[:, c, lms],
-                                rhs=w_codes[:, c, cols].bitcast(FP8X4),
-                                rhs_scale=w_scales[:, c, cols],
-                                start=(c == 0),
-                                stop=(c == CH_PASSES - 1),
-                            )
-                    nc.vector.tensor_tensor(
-                        out=kv_grp[:, P * ct : P * (ct + 1), :],
-                        in0=acc[:].rearrange("p t n -> p n t"),
-                        in1=bias[:, cols].unsqueeze(2).to_broadcast([P, P, PACK]),
-                        op=ADD,
-                    )
-                quantise(nc, kv_codes[:, g, :], kv_scales[:, g, :], kv_grp[:])
-                for j in range(3):
-                    rows = slice(P * j, P * (j + 1))
-                    nc.tensor.matmul_mx(
-                        out=comp[j][:],
-                        lhsT=e_codes[r // 2][:, g, rows].bitcast(FP8X4),
-                        lhsT_scale=e_scales[r // 2][:, g, rows],
-                        rhs=kv_codes[:, g, :].bitcast(FP8X4),
-                        rhs_scale=kv_scales[:, g, :],
-                        start=(g == 0),
-                        stop=(g == LM_PASSES - 1),
-                    )
-            heads = slice(4 * (r % 2), 4 * (r % 2) + 4)
-            for j in range(3):
-                result = out_stage.tile([P, RANGE], F32)
-                nc.scalar.copy(out=result[:], in_=comp[j][:])
-                nc.sync.dma_start(
-                    out=outs[r // 2][0, heads, P * j : P * (j + 1), :].rearrange("h j d -> j h d"),
-                    in_=result[:].rearrange("p (h d) -> p h d", d=HEAD),
+
+        def compress(r, j):
+            h = r // 2
+            rows = slice(P * j, P * (j + 1))
+            comp = side_banks.tile([P, RANGE], F32, tag="side")
+            for g in range(GROUPS):
+                nc.tensor.matmul_mx(
+                    out=comp[:],
+                    lhsT=e_codes[h][:, g, rows].bitcast(FP8X4),
+                    lhsT_scale=e_scales[h][:, g, rows],
+                    rhs=kv_codes[r][:, g, :].bitcast(FP8X4),
+                    rhs_scale=kv_scales[r][:, g, :],
+                    start=(g == 0),
+                    stop=(g == GROUPS - 1),
                 )
+            result = out_stage.tile([P, RANGE], F32)
+            nc.scalar.copy(out=result[:], in_=comp[:])
+            heads = slice(4 * (r % 2), 4 * (r % 2) + 4)
+            nc.sync.dma_start(
+                out=outs[h][0, heads, rows, :].rearrange("h j d -> j h d"),
+                in_=result[:].rearrange("p (h d) -> p h d", d=HEAD),
+            )
+
+        both = [nc.vector.tensor_copy, nc.scalar.copy]
+        scalar_only = [nc.scalar.copy, nc.scalar.copy]
+        vector_only = [nc.vector.tensor_copy, nc.vector.tensor_copy]
+
+        regroup_weights(0, both)
+        quantise_weights(0)
+        for t in range(PACK):
+            pool_landmarks(0, t, [nc.scalar.copy, nc.vector.tensor_copy])
+        quantise_landmarks(0)
+        for ct in range(BANKS):
+            multiply(0, ct)
+
+        emptied = None
+        for u in range(len(UNITS) + 3):
+            for r in range(1, RANGES):
+                first = UNITS.index((r, 0))
+                if u == max(first - 3, 0):
+                    regroup_weights(r, vector_only if first == 1 else scalar_only)
+                if u == first - 1:
+                    quantise_weights(r)
+            for g in range(1, GROUPS):
+                if u == UNITS.index((0, g)) - 1:
+                    quantise_landmarks(g)
+            for h in range(2):
+                needed = UNITS.index((2 * h, GROUPS - 1)) + 2
+                if u == needed - 2:
+                    regroup_compressor(h)
+                if u == needed:
+                    quantise_compressor(h)
+            for ct in range(BANKS):
+                before = emptied
+                emptied = drain(u, ct) if u < len(UNITS) else None
+                if before is not None:
+                    quantise_bank(*before)
+                if u + 1 < len(UNITS):
+                    multiply(u + 1, ct)
+                for g in range(1, GROUPS):
+                    if u == UNITS.index((0, g)) - 2:
+                        pool_landmarks(g, ct, scalar_only)
+                for r in range(RANGES):
+                    if u == UNITS.index((r, GROUPS - 1)) + 2 and ct > 0:
+                        compress(r, ct - 1)

@@ -54,7 +54,6 @@ def tile_efficientmultiscaledilatedattention_pa_kernel(
 ):
     nc = tc.nc
     with ExitStack() as ctx:
-        ctx.enter_context(tc.manual_schedule())
         keep = ctx.enter_context(tc.tile_pool(name="keep", bufs=1))
         w_stage = ctx.enter_context(tc.tile_pool(name="w_stage", bufs=4))
         e_stage = ctx.enter_context(tc.tile_pool(name="e_stage", bufs=3))

@@ -196,7 +196,7 @@ def tile_efficientmultiscaledilatedattention_pa_kernel(
                         [P, K_PASS, PACK], BF16, align_bytes=64, name="xl_grp"
                     )
                 xl_grp = xl_grouped[(g, c)]
-                mean = side_banks.tile([P, PACK, P], F32, tag="side")
+                mean = side_banks.tile([P, PACK, P], BF16, tag="side")
                 for s in range(PACK):
                     chans = slice(K_PASS * c + P * s, K_PASS * c + P * (s + 1))
                     for e in range(2):

@@ -27,9 +27,18 @@ RANGES = KV // RANGE
 BANKS = RANGE // P
 OUT_TILES = COMPRESSED // P
 HALF = P // 2
+LM_TILES = LANDMARKS // P
 MAIN_TILES = 9
 
-UNITS = [(r, g) for g in range(GROUPS) for r in (0, 1)] + [(r, g) for r in (2, 3) for g in range(GROUPS)]
+LOADS = [("w",0),("x",0),("x",1),("x",2),("x",3),("w",1),("x",4),("x",5),("x",6),("x",7),("w",2),("x",8),("t",0),("e",0),("w",3),("e",1)]
+MULT = mybir.AluOpType.mult
+HEADP = ["R0"]
+WENG = ["vs", "ss", "ss", "ss"]
+XENG = "svsvssssssss"
+EENG = ["sss", "sss"]
+XQ = 2
+POS = {"R1": 0, "P4": 1, "P5": 2, "P6": 3, "P7": 4, "R2": 8, "P8": 13, "P9": 14, "P10": 15, "P11": 16, "E0": 24, "R3": 26, "E1": 34}
+UNITS = [(0, 0), (1, 0), (0, 1), (1, 1), (2, 0), (2, 1), (0, 2), (1, 2), (2, 2), (3, 0), (3, 1), (3, 2)]
 
 FLOPS = 2 * LANDMARKS * CHANNELS * KV + 2 * 2 * COMPRESSED * LANDMARKS * CHANNELS
 
@@ -55,10 +64,11 @@ def tile_efficientmultiscaledilatedattention_pa_kernel(
     nc = tc.nc
     with ExitStack() as ctx:
         keep = ctx.enter_context(tc.tile_pool(name="keep", bufs=1))
-        w_stage = ctx.enter_context(tc.tile_pool(name="w_stage", bufs=4))
-        e_stage = ctx.enter_context(tc.tile_pool(name="e_stage", bufs=3))
-        xl_stage = ctx.enter_context(tc.tile_pool(name="xl_stage", bufs=4))
-        kv_stage = ctx.enter_context(tc.tile_pool(name="kv_stage", bufs=4))
+        w_pool = ctx.enter_context(tc.tile_pool(name="w_pool", bufs=3))
+        w_stage = ctx.enter_context(tc.tile_pool(name="w_stage", bufs=2))
+        e_stage = ctx.enter_context(tc.tile_pool(name="e_stage", bufs=1))
+        xl_stage = ctx.enter_context(tc.tile_pool(name="xl_stage", bufs=2))
+        kv_stage = ctx.enter_context(tc.tile_pool(name="kv_stage", bufs=3))
         kv_keep = ctx.enter_context(tc.tile_pool(name="kv_keep", bufs=3))
         out_stage = ctx.enter_context(tc.tile_pool(name="out_stage", bufs=4))
         acc_banks = ctx.enter_context(tc.psum_pool(name="acc_banks", bufs=BANKS))
@@ -68,12 +78,15 @@ def tile_efficientmultiscaledilatedattention_pa_kernel(
         nc.sync.dma_start(out=bias_in[:], in_=b_kv.unsqueeze(0))
 
         w_view = W_kv.rearrange("(s p) n -> p s n", p=P)
-        w_raw = [
-            keep.tile([P, CH_PASSES * PACK, RANGE], BF16, name="w_raw%d" % r) for r in range(RANGES)
-        ]
+        w_raw = []
 
         def load_weights(r):
-            nc.sync.dma_start(out=w_raw[r][:], in_=w_view[:, :, RANGE * r : RANGE * (r + 1)])
+            w_raw.append(w_pool.tile([P, CH_PASSES * PACK, RANGE], BF16, name="w_raw"))
+            for c in range(CH_PASSES):
+                slots = slice(PACK * c, PACK * (c + 1))
+                nc.sync.dma_start(
+                    out=w_raw[r][:, slots, :], in_=w_view[:, slots, RANGE * r : RANGE * (r + 1)]
+                )
 
         tokens = x.flatten_outer_dims()
         token_tiles = []
@@ -86,29 +99,42 @@ def tile_efficientmultiscaledilatedattention_pa_kernel(
             )
             token_tiles.extend([x_main[:, 0, :], x_main[:, 1, :]])
 
-        load_weights(0)
-        for m in range(PACK):
-            load_main(m)
-        load_weights(1)
-        for m in range(PACK, MAIN_TILES):
-            load_main(m)
-
         x_tail = keep.tile([P, 6, CHANNELS], BF16)
-        by_two = tokens.rearrange("(k b r c e) d -> b r e c k d", k=6, b=4, r=2, c=24, e=2)
-        for b in range(4):
-            nc.sync.dma_start(out=x_tail[b:96:4, :, :], in_=by_two[b, 0, 0])
-        by_three = tokens.rearrange("(k b r c e) d -> b r e c k d", k=8, b=2, r=3, c=16, e=3)
-        for b in range(2):
-            nc.sync.dma_start(out=x_tail[96 + b : P : 2, :, :], in_=by_three[b, 0, 0][:, 0:6, :])
-        token_tiles.extend([x_tail[:, k, :] for k in range(6)])
+
+        def load_tail():
+            by_two = tokens.rearrange("(k b r c e) d -> b r e c k d", k=6, b=4, r=2, c=24, e=2)
+            for b in range(4):
+                nc.sync.dma_start(out=x_tail[b:96:4, :, :], in_=by_two[b, 0, 0])
+            by_three = tokens.rearrange("(k b r c e) d -> b r e c k d", k=8, b=2, r=3, c=16, e=3)
+            for b in range(2):
+                nc.sync.dma_start(out=x_tail[96 + b : P : 2, :, :], in_=by_three[b, 0, 0][:, 0:6, :])
+            token_tiles.extend([x_tail[:, k, :] for k in range(6)])
 
         e_raw = [
-            keep.tile([P, GROUPS * PACK, COMPRESSED], BF16, name="e_raw%d" % h) for h in range(2)
+            keep.tile([P, LM_TILES, COMPRESSED], BF16, name="e_raw%d" % h) for h in range(2)
         ]
-        load_weights(2)
-        nc.sync.dma_start(out=e_raw[0][:], in_=E_k.rearrange("(s p) j -> p s j", p=P))
-        load_weights(3)
-        nc.sync.dma_start(out=e_raw[1][:], in_=E_v.rearrange("(s p) j -> p s j", p=P))
+
+        def load_compressor(h):
+            rows = (E_k, E_v)[h]
+            nc.sync.dma_start(
+                out=e_raw[h][:, 0:MAIN_TILES, :],
+                in_=rows[0 : P * MAIN_TILES, :].rearrange("(s p) j -> p s j", p=P),
+            )
+            two = rows[1152:1440, :].rearrange("(v e j) n -> e j v n", v=3, e=2)
+            three = rows[1440:1536, :].rearrange("(v e j) n -> e j v n", v=3, e=2)
+            for e in range(2):
+                nc.sync.dma_start(out=e_raw[h][HALF * e : HALF * e + 48, MAIN_TILES:, :], in_=two[e])
+                nc.sync.dma_start(out=e_raw[h][HALF * e + 48 : HALF * (e + 1), MAIN_TILES:, :], in_=three[e])
+
+        for what, i in LOADS:
+            if what == "w":
+                load_weights(i)
+            if what == "x":
+                load_main(i)
+            if what == "t":
+                load_tail()
+            if what == "e":
+                load_compressor(i)
 
         ident = keep.tile([P, P], BF16)
         make_identity(nc, ident[:])
@@ -136,204 +162,238 @@ def tile_efficientmultiscaledilatedattention_pa_kernel(
         ones = keep.tile([P, P], BF16)
         nc.vector.memset(ones[:], 1.0)
         bias_row = keep.tile([P, KV], BF16)
-        nc.vector.memset(bias_row[:], 0.0)
+        nc.gpsimd.memset(bias_row[:], 0.0)
         nc.vector.tensor_copy(out=bias_row[0:1, :], in_=bias_in[:])
         bias = keep.tile([P, KV], BF16)
-        for r in range(RANGES):
+
+        def spread_bias(r):
             cols = slice(RANGE * r, RANGE * (r + 1))
-            spread = side_banks.tile([P, RANGE], F32, tag="side")
+            spread = side_banks.tile([P, RANGE], F32, tag="side", name="side")
             nc.tensor.matmul(out=spread[:], lhsT=ones[:], rhs=bias_row[:, cols], start=True, stop=True)
             nc.scalar.copy(out=bias[:, cols], in_=spread[:])
 
-        w_codes = keep.tile([P, CH_PASSES, KV], U32, align_bytes=64)
-        w_scales = keep.tile([P, CH_PASSES, KV], U8, align_bytes=64)
-        xl_codes = keep.tile([P, CH_PASSES, LANDMARKS], U32, align_bytes=64)
-        xl_scales = keep.tile([P, CH_PASSES, LANDMARKS], U8, align_bytes=64)
+        w_codes = [
+            keep.tile([P, CH_PASSES, RANGE], U32, align_bytes=64, name="w_codes%d" % r)
+            for r in range(RANGES)
+        ]
+        w_scales = [
+            keep.tile([P, CH_PASSES, RANGE], U8, align_bytes=64, name="w_scales%d" % r)
+            for r in range(RANGES)
+        ]
+        xl_codes = keep.tile([P, LM_TILES, CH_PASSES, P], U32, align_bytes=64)
+        xl_scales = keep.tile([P, LM_TILES, CH_PASSES, P], U8, align_bytes=64)
         e_codes = [
-            keep.tile([P, GROUPS, COMPRESSED], U32, align_bytes=64, name="e_codes%d" % h)
+            keep.tile([P, GROUPS * COMPRESSED], U32, align_bytes=64, name="e_codes%d" % h)
             for h in range(2)
         ]
         e_scales = [
-            keep.tile([P, GROUPS, COMPRESSED], U8, align_bytes=64, name="e_scales%d" % h)
+            keep.tile([P, GROUPS * COMPRESSED], U8, align_bytes=64, name="e_scales%d" % h)
             for h in range(2)
         ]
 
         w_grouped = {}
 
         def regroup_weights(r, copies):
+            w_grouped[r] = w_stage.tile([P, CH_PASSES, RANGE, PACK], BF16, align_bytes=64, name="w_grp")
             for c in range(CH_PASSES):
-                w_grp = w_stage.tile([P, RANGE, PACK], BF16, align_bytes=64)
-                regroup(copies[c], w_grp[:], w_raw[r][:, PACK * c : PACK * (c + 1), :])
-                w_grouped[(r, c)] = w_grp
+                regroup(copies[c], w_grouped[r][:, c, :, :], w_raw[r][:, PACK * c : PACK * (c + 1), :])
 
-        def quantise_weights(r):
-            cols = slice(RANGE * r, RANGE * (r + 1))
-            for c in range(CH_PASSES):
-                quantise(nc, w_codes[:, c, cols], w_scales[:, c, cols], w_grouped[(r, c)][:])
+        def quantise_weights(r, whole):
+            if whole:
+                quantise(
+                    nc,
+                    w_codes[r][:].rearrange("p c n -> p (c n)"),
+                    w_scales[r][:].rearrange("p c n -> p (c n)"),
+                    w_grouped[r][:].rearrange("p c n t -> p (c n) t"),
+                )
+            else:
+                for c in range(CH_PASSES):
+                    quantise(nc, w_codes[r][:, c, :], w_scales[r][:, c, :], w_grouped[r][:, c, :, :])
 
         e_grouped = {}
 
         def regroup_compressor(h):
+            e_grouped[h] = e_stage.tile([P, GROUPS * COMPRESSED, PACK], BF16, align_bytes=64, name="e_grp")
             for g in range(GROUPS):
-                e_grp = e_stage.tile([P, COMPRESSED, PACK], BF16, align_bytes=64)
-                regroup(nc.scalar.copy, e_grp[:], e_raw[h][:, PACK * g : PACK * (g + 1), :])
-                e_grouped[(h, g)] = e_grp
+                regroup(
+                    eng[EENG[h][g]],
+                    e_grouped[h][:, COMPRESSED * g : COMPRESSED * (g + 1), :],
+                    e_raw[h][:, PACK * g : PACK * (g + 1), :],
+                )
 
         def quantise_compressor(h):
-            for g in range(GROUPS):
-                for lo, hi in ((0, 256), (256, 384)):
-                    quantise(
-                        nc, e_codes[h][:, g, lo:hi], e_scales[h][:, g, lo:hi], e_grouped[(h, g)][:, lo:hi, :]
-                    )
+            for lo, hi in ((0, 1024), (1024, 1152)):
+                quantise(nc, e_codes[h][:, lo:hi], e_scales[h][:, lo:hi], e_grouped[h][:, lo:hi, :])
 
         xl_grouped = {}
 
-        def pool_landmarks(g, t, copies):
-            m = PACK * g + t
+        def pool_landmarks(m, copy):
+            g, t = m // PACK, m % PACK
+            if t == 0:
+                xl_grouped[g] = xl_stage.tile(
+                    [P, PACK, CH_PASSES, P, PACK], BF16, align_bytes=64, name="xl_grp"
+                )
+            mean = side_banks.tile([P, CH_PASSES, PACK, P], BF16, tag="side", name="side")
             for c in range(CH_PASSES):
-                if t == 0:
-                    xl_grouped[(g, c)] = xl_stage.tile(
-                        [P, K_PASS, PACK], BF16, align_bytes=64, name="xl_grp"
-                    )
-                xl_grp = xl_grouped[(g, c)]
-                mean = side_banks.tile([P, PACK, P], BF16, tag="side")
                 for s in range(PACK):
                     chans = slice(K_PASS * c + P * s, K_PASS * c + P * (s + 1))
                     for e in range(2):
                         nc.tensor.matmul(
-                            out=mean[:, s, HALF * e : HALF * (e + 1)],
+                            out=mean[:, c, s, HALF * e : HALF * (e + 1)],
                             lhsT=token_tiles[2 * m + e][:, chans],
                             rhs=(main_mat if m < MAIN_TILES else tail_mat)[:],
                             start=True,
                             stop=True,
                         )
-                if m < MAIN_TILES:
-                    copies[c](
-                        out=xl_grp[:, P * t : P * (t + 1), :], in_=mean[:].rearrange("p s l -> p l s")
-                    )
-                else:
-                    v = m - MAIN_TILES
-                    halves = mean[:].rearrange("p s (e j) -> p e j s", e=2)
-                    first = P + 96 * v
-                    copies[c](
-                        out=xl_grp[:, first : first + 96, :].rearrange("p (e j) s -> p e j s", e=2),
-                        in_=halves[:, :, 0:48, :],
-                    )
-                    first = P + 288 + 32 * v
-                    copies[c](
-                        out=xl_grp[:, first : first + 32, :].rearrange("p (e j) s -> p e j s", e=2),
-                        in_=halves[:, :, 48:64, :],
-                    )
+            copy(out=xl_grouped[g][:, t, :, :, :], in_=mean[:].rearrange("p c s l -> p c l s"))
 
-        def quantise_landmarks(g):
-            lms = slice(K_PASS * g, K_PASS * (g + 1))
-            for c in range(CH_PASSES):
-                quantise(nc, xl_codes[:, c, lms], xl_scales[:, c, lms], xl_grouped[(g, c)][:])
+        def quantise_landmarks(lo, hi):
+            g = lo // PACK
+            quantise(
+                nc,
+                xl_codes[:, lo:hi, :, :].rearrange("p m c l -> p (m c l)"),
+                xl_scales[:, lo:hi, :, :].rearrange("p m c l -> p (m c l)"),
+                xl_grouped[g][:, lo - PACK * g : hi - PACK * g, :, :, :].rearrange("p m c l s -> p (m c l) s"),
+            )
 
         acc = {}
         kv_codes = {}
         kv_scales = {}
 
-        def multiply(u, ct):
+        def open_bank(u, ct):
+            acc[(u, ct)] = acc_banks.tile([P, PACK, P], F32, tag="acc", name="acc")
+
+        def multiply(u, ct, t):
             r, g = UNITS[u]
-            cols = slice(RANGE * r + P * ct, RANGE * r + P * (ct + 1))
-            bank = acc_banks.tile([P, PACK, P], F32, tag="acc")
-            for t in range(PACK):
-                lms = slice(K_PASS * g + P * t, K_PASS * g + P * (t + 1))
-                for c in range(CH_PASSES):
-                    nc.tensor.matmul_mx(
-                        out=bank[:, t, :],
-                        lhsT=xl_codes[:, c, lms].bitcast(FP8X4),
-                        lhsT_scale=xl_scales[:, c, lms],
-                        rhs=w_codes[:, c, cols].bitcast(FP8X4),
-                        rhs_scale=w_scales[:, c, cols],
-                        start=(c == 0),
-                        stop=(c == CH_PASSES - 1),
-                    )
-            acc[(u, ct)] = bank
+            cols = slice(P * ct, P * (ct + 1))
+            m = PACK * g + t
+            for c in range(CH_PASSES):
+                nc.tensor.matmul_mx(
+                    out=acc[(u, ct)][:, t, :],
+                    lhsT=xl_codes[:, m, c, :].bitcast(FP8X4),
+                    lhsT_scale=xl_scales[:, m, c, :],
+                    rhs=w_codes[r][:, c, cols].bitcast(FP8X4),
+                    rhs_scale=w_scales[r][:, c, cols],
+                    start=(c == 0),
+                    stop=(c == CH_PASSES - 1),
+                )
+
+        kv_grouped = {}
 
         def drain(u, ct):
             r, g = UNITS[u]
-            if g == 0 and ct == 0:
-                kv_codes[r] = kv_keep.tile([P, GROUPS, RANGE], U32, align_bytes=64, name="kv_codes")
-                kv_scales[r] = kv_keep.tile([P, GROUPS, RANGE], U8, align_bytes=64, name="kv_scales")
+            if ct == 0:
+                kv_grouped[u] = kv_stage.tile([P, RANGE, PACK], BF16, align_bytes=64, name="kv_grp")
             cols = slice(RANGE * r + P * ct, RANGE * r + P * (ct + 1))
-            kv_grp = kv_stage.tile([P, P, PACK], BF16, align_bytes=64)
             nc.vector.tensor_tensor(
-                out=kv_grp[:],
+                out=kv_grouped[u][:, P * ct : P * (ct + 1), :],
                 in0=acc[(u, ct)][:].rearrange("p t n -> p n t"),
                 in1=bias[:, cols].unsqueeze(2).to_broadcast([P, P, PACK]),
                 op=ADD,
             )
-            return (r, g, ct, kv_grp)
 
-        def quantise_bank(r, g, ct, kv_grp):
-            part = slice(P * ct, P * (ct + 1))
-            quantise(nc, kv_codes[r][:, g, part], kv_scales[r][:, g, part], kv_grp[:])
+        def quantise_unit(u, lo, hi):
+            r, g = UNITS[u]
+            if r not in kv_codes:
+                kv_codes[r] = kv_keep.tile([P, GROUPS, RANGE], U32, align_bytes=64, name="kv_codes")
+                kv_scales[r] = kv_keep.tile([P, GROUPS, RANGE], U8, align_bytes=64, name="kv_scales")
+            quantise(nc, kv_codes[r][:, g, lo:hi], kv_scales[r][:, g, lo:hi], kv_grouped[u][:, lo:hi, :])
 
         outs = [out_0, out_1]
 
-        def compress(r, j):
+        def compress(r, ct):
             h = r // 2
-            rows = slice(P * j, P * (j + 1))
-            comp = side_banks.tile([P, RANGE], F32, tag="side")
+            part = slice(P * ct, P * (ct + 1))
+            comp = side_banks.tile([P, OUT_TILES, HEAD], F32, tag="side", name="side")
+            for j in range(OUT_TILES):
+                for g in range(GROUPS):
+                    rows = slice(COMPRESSED * g + P * j, COMPRESSED * g + P * (j + 1))
+                    nc.tensor.matmul_mx(
+                        out=comp[:, j, :],
+                        lhsT=e_codes[h][:, rows].bitcast(FP8X4),
+                        lhsT_scale=e_scales[h][:, rows],
+                        rhs=kv_codes[r][:, g, part].bitcast(FP8X4),
+                        rhs_scale=kv_scales[r][:, g, part],
+                        start=(g == 0),
+                        stop=(g == GROUPS - 1),
+                    )
+            result = out_stage.tile([P, OUT_TILES, HEAD], F32, name="result")
+            nc.scalar.copy(out=result[:], in_=comp[:])
+            nc.sync.dma_start(
+                out=outs[h][0, 4 * (r % 2) + ct, :, :].rearrange("(j p) d -> p j d", p=P),
+                in_=result[:],
+            )
+
+        def compress_wide(r, j):
+            h = r // 2
+            comp = side_banks.tile([P, RANGE], F32, tag="side", name="side")
             for g in range(GROUPS):
+                rows = slice(COMPRESSED * g + P * j, COMPRESSED * g + P * (j + 1))
                 nc.tensor.matmul_mx(
                     out=comp[:],
-                    lhsT=e_codes[h][:, g, rows].bitcast(FP8X4),
-                    lhsT_scale=e_scales[h][:, g, rows],
+                    lhsT=e_codes[h][:, rows].bitcast(FP8X4),
+                    lhsT_scale=e_scales[h][:, rows],
                     rhs=kv_codes[r][:, g, :].bitcast(FP8X4),
                     rhs_scale=kv_scales[r][:, g, :],
                     start=(g == 0),
                     stop=(g == GROUPS - 1),
                 )
-            result = out_stage.tile([P, RANGE], F32)
+            result = out_stage.tile([P, RANGE], F32, name="result")
             nc.scalar.copy(out=result[:], in_=comp[:])
             heads = slice(4 * (r % 2), 4 * (r % 2) + 4)
             nc.sync.dma_start(
-                out=outs[h][0, heads, rows, :].rearrange("h j d -> j h d"),
+                out=outs[h][0, heads, P * j : P * (j + 1), :].rearrange("h j d -> j h d"),
                 in_=result[:].rearrange("p (h d) -> p h d", d=HEAD),
             )
 
-        both = [nc.vector.tensor_copy, nc.scalar.copy]
-        scalar_only = [nc.scalar.copy, nc.scalar.copy]
-        vector_only = [nc.vector.tensor_copy, nc.vector.tensor_copy]
+        eng = {"v": nc.vector.tensor_copy, "s": nc.scalar.copy, "g": lambda out, in_: nc.gpsimd.tensor_scalar(out=out, in0=in_, scalar1=1.0, scalar2=0.0, op0=MULT, op1=ADD)}
 
-        regroup_weights(0, both)
-        quantise_weights(0)
-        for t in range(PACK):
-            pool_landmarks(0, t, [nc.scalar.copy, nc.vector.tensor_copy])
-        quantise_landmarks(0)
+        def prep(a):
+            k, i = a[0], int(a[1:])
+            if k == "R":
+                spread_bias(i)
+                regroup_weights(i, [eng[z] for z in WENG[i]])
+                quantise_weights(i, i > 0)
+            if k == "P":
+                pool_landmarks(i, eng[XENG[i]])
+                if i < 4:
+                    quantise_landmarks(i, i + 1)
+                elif i % XQ == XQ - 1:
+                    quantise_landmarks(i - XQ + 1, i + 1)
+            if k == "E":
+                regroup_compressor(i)
+                quantise_compressor(i)
+
+        for a in HEADP:
+            prep(a)
         for ct in range(BANKS):
-            multiply(0, ct)
-
-        emptied = None
-        for u in range(len(UNITS) + 3):
-            for r in range(1, RANGES):
-                first = UNITS.index((r, 0))
-                if u == max(first - 3, 0):
-                    regroup_weights(r, vector_only if first == 1 else scalar_only)
-                if u == first - 1:
-                    quantise_weights(r)
-            for g in range(1, GROUPS):
-                if u == UNITS.index((0, g)) - 1:
-                    quantise_landmarks(g)
-            for h in range(2):
-                needed = UNITS.index((2 * h, GROUPS - 1)) + 2
-                if u == needed - 2:
-                    regroup_compressor(h)
-                if u == needed:
-                    quantise_compressor(h)
+            open_bank(0, ct)
+        for t in range(PACK):
+            prep("P%d" % t)
             for ct in range(BANKS):
-                before = emptied
-                emptied = drain(u, ct) if u < len(UNITS) else None
-                if before is not None:
-                    quantise_bank(*before)
-                if u + 1 < len(UNITS):
-                    multiply(u + 1, ct)
-                for g in range(1, GROUPS):
-                    if u == UNITS.index((0, g)) - 2:
-                        pool_landmarks(g, ct, scalar_only)
+                multiply(0, ct, t)
+        LAST = len(UNITS) - 1
+        for u in range(len(UNITS) + 2):
+            for ct in range(BANKS):
+                for a, pos in POS.items():
+                    if pos == 4 * u + ct:
+                        prep(a)
+                if u <= LAST:
+                    drain(u, ct)
+                if ct == 0 and 0 < u <= LAST:
+                    quantise_unit(u - 1, 0, RANGE)
+                if u == LAST and ct > 0:
+                    quantise_unit(u, P * (ct - 1), P * ct)
+                if u == LAST + 1 and ct == 0:
+                    quantise_unit(LAST, RANGE - P, RANGE)
+                if u + 1 <= LAST:
+                    open_bank(u + 1, ct)
+                    for t in range(PACK):
+                        multiply(u + 1, ct, t)
                 for r in range(RANGES):
-                    if u == UNITS.index((r, GROUPS - 1)) + 2 and ct > 0:
-                        compress(r, ct - 1)
+                    last = max(i for i in range(12) if UNITS[i][0] == r)
+                    if last == LAST:
+                        if u == LAST + 1:
+                            compress(r, ct)
+                    elif u == last + 2 and ct > 0:
+                        compress_wide(r, ct - 1)

@@ -28,17 +28,29 @@ BANKS = RANGE // P
 OUT_TILES = COMPRESSED // P
 HALF = P // 2
 LM_TILES = LANDMARKS // P
+GRID = 48
 MAIN_TILES = 9
 
-LOADS = [("w",0),("x",0),("x",1),("x",2),("x",3),("w",1),("x",4),("x",5),("x",6),("x",7),("w",2),("x",8),("t",0),("e",0),("w",3),("e",1)]
+LOADS = [("x", 0), ("x", 1), ("w", 0), ("x", 2), ("x", 3), ("w", 1), ("x", 4), ("x", 5), ("w", 2), ("x", 6), ("x", 7), ("e", 0), ("x", 8), ("t", 0), ("e", 1), ("w", 3)]
 MULT = mybir.AluOpType.mult
-HEADP = ["R0"]
-WENG = ["vs", "ss", "ss", "ss"]
-XENG = "svsvssssssss"
+HEADP = ["R0", "P0", "P1", "P2", "P3"]
+WENG = ["vv", "vs", "vs", "ss"]
+XENG = "ssssssssssss"
 EENG = ["sss", "sss"]
 XQ = 2
-POS = {"R1": 0, "P4": 1, "P5": 2, "P6": 3, "P7": 4, "R2": 8, "P8": 13, "P9": 14, "P10": 15, "P11": 16, "E0": 24, "R3": 26, "E1": 34}
-UNITS = [(0, 0), (1, 0), (0, 1), (1, 1), (2, 0), (2, 1), (0, 2), (1, 2), (2, 2), (3, 0), (3, 1), (3, 2)]
+POS = {"R1": 0, "R2": 4, "P4": 4, "P5": 5, "P6": 6, "P7": 7, "P8": 12, "T0": 13, "E0": 26, "R3": 28, "E1": 34}
+def two_runs(i):
+    runs = []
+    for row in range(0, GRID, 2):
+        lo, hi = max(0, GRID * row - P * i), min(P, GRID * (row + 1) - P * i)
+        if lo < hi:
+            runs.append((lo, hi))
+    return runs
+
+
+TWO_RUNS = [two_runs(k) for k in range(3)]
+TWO_COUNT = [sum(hi - lo for lo, hi in runs) // 4 for runs in TWO_RUNS]
+UNITS = [(0, 0), (1, 0), (2, 0), (0, 1), (1, 1), (2, 1), (0, 2), (1, 2), (2, 2), (3, 0), (3, 1), (3, 2)]
 
 FLOPS = 2 * LANDMARKS * CHANNELS * KV + 2 * 2 * COMPRESSED * LANDMARKS * CHANNELS
 
@@ -64,11 +76,10 @@ def tile_efficientmultiscaledilatedattention_pa_kernel(
     nc = tc.nc
     with ExitStack() as ctx:
         keep = ctx.enter_context(tc.tile_pool(name="keep", bufs=1))
-        w_pool = ctx.enter_context(tc.tile_pool(name="w_pool", bufs=3))
         w_stage = ctx.enter_context(tc.tile_pool(name="w_stage", bufs=2))
         e_stage = ctx.enter_context(tc.tile_pool(name="e_stage", bufs=1))
         xl_stage = ctx.enter_context(tc.tile_pool(name="xl_stage", bufs=2))
-        kv_stage = ctx.enter_context(tc.tile_pool(name="kv_stage", bufs=3))
+        kv_stage = ctx.enter_context(tc.tile_pool(name="kv_stage", bufs=2))
         kv_keep = ctx.enter_context(tc.tile_pool(name="kv_keep", bufs=3))
         out_stage = ctx.enter_context(tc.tile_pool(name="out_stage", bufs=4))
         acc_banks = ctx.enter_context(tc.psum_pool(name="acc_banks", bufs=BANKS))
@@ -76,12 +87,16 @@ def tile_efficientmultiscaledilatedattention_pa_kernel(
 
         bias_in = keep.tile([1, KV], BF16)
         nc.sync.dma_start(out=bias_in[:], in_=b_kv.unsqueeze(0))
+        bias_row = keep.tile([P, KV], BF16)
+        nc.vector.memset(bias_row[:], 0.0)
+        nc.vector.tensor_copy(out=bias_row[0:1, :], in_=bias_in[:])
 
         w_view = W_kv.rearrange("(s p) n -> p s n", p=P)
-        w_raw = []
+        w_raw = [
+            keep.tile([P, CH_PASSES * PACK, RANGE], BF16, name="w_raw%d" % r) for r in range(RANGES)
+        ]
 
         def load_weights(r):
-            w_raw.append(w_pool.tile([P, CH_PASSES * PACK, RANGE], BF16, name="w_raw"))
             for c in range(CH_PASSES):
                 slots = slice(PACK * c, PACK * (c + 1))
                 nc.sync.dma_start(
@@ -99,32 +114,19 @@ def tile_efficientmultiscaledilatedattention_pa_kernel(
             )
             token_tiles.extend([x_main[:, 0, :], x_main[:, 1, :]])
 
-        x_tail = keep.tile([P, 6, CHANNELS], BF16)
+        x_three = keep.tile([P, 2, CHANNELS], BF16)
 
         def load_tail():
-            by_two = tokens.rearrange("(k b r c e) d -> b r e c k d", k=6, b=4, r=2, c=24, e=2)
-            for b in range(4):
-                nc.sync.dma_start(out=x_tail[b:96:4, :, :], in_=by_two[b, 0, 0])
-            by_three = tokens.rearrange("(k b r c e) d -> b r e c k d", k=8, b=2, r=3, c=16, e=3)
-            for b in range(2):
-                nc.sync.dma_start(out=x_tail[96 + b : P : 2, :, :], in_=by_three[b, 0, 0][:, 0:6, :])
-            token_tiles.extend([x_tail[:, k, :] for k in range(6)])
+            by_three = tokens.rearrange("(k b r c e) d -> b r e c k d", k=2, b=8, r=3, c=16, e=3)
+            for b in range(8):
+                nc.sync.dma_start(out=x_three[16 * b : 16 * (b + 1), :, :], in_=by_three[b, 0, 0])
 
         e_raw = [
             keep.tile([P, LM_TILES, COMPRESSED], BF16, name="e_raw%d" % h) for h in range(2)
         ]
 
         def load_compressor(h):
-            rows = (E_k, E_v)[h]
-            nc.sync.dma_start(
-                out=e_raw[h][:, 0:MAIN_TILES, :],
-                in_=rows[0 : P * MAIN_TILES, :].rearrange("(s p) j -> p s j", p=P),
-            )
-            two = rows[1152:1440, :].rearrange("(v e j) n -> e j v n", v=3, e=2)
-            three = rows[1440:1536, :].rearrange("(v e j) n -> e j v n", v=3, e=2)
-            for e in range(2):
-                nc.sync.dma_start(out=e_raw[h][HALF * e : HALF * e + 48, MAIN_TILES:, :], in_=two[e])
-                nc.sync.dma_start(out=e_raw[h][HALF * e + 48 : HALF * (e + 1), MAIN_TILES:, :], in_=three[e])
+            nc.sync.dma_start(out=e_raw[h][:], in_=(E_k, E_v)[h].rearrange("(s p) j -> p s j", p=P))
 
         for what, i in LOADS:
             if what == "w":
@@ -140,30 +142,31 @@ def tile_efficientmultiscaledilatedattention_pa_kernel(
         make_identity(nc, ident[:])
         half_ident = keep.tile([P, P], BF16)
         nc.vector.tensor_scalar_mul(out=half_ident[:], in0=ident[:], scalar1=0.5)
-        main_mat = keep.tile([P, HALF], BF16)
-        pairs = half_ident[:].rearrange("p (j e) -> p j e", e=2)
-        nc.vector.tensor_tensor(out=main_mat[:], in0=pairs[:, :, 0], in1=pairs[:, :, 1], op=ADD)
-        tail_mat = keep.tile([P, HALF], BF16)
-        two = half_ident[:, 0:96].rearrange("p (u e b) -> p b u e", u=12, e=2, b=4)
-        nc.vector.tensor_tensor(
-            out=tail_mat[:, 0:48].rearrange("p (b u) -> p b u", b=4),
-            in0=two[:, :, :, 0],
-            in1=two[:, :, :, 1],
-            op=ADD,
-        )
-        three = half_ident[:, 96:P].rearrange("p (u e b) -> p b u e", u=8, e=2, b=2)
-        nc.vector.tensor_tensor(
-            out=tail_mat[:, 48:64].rearrange("p (b u) -> p b u", b=2),
-            in0=three[:, :, :, 0],
-            in1=three[:, :, :, 1],
-            op=ADD,
-        )
+        pool_mats = []
+        for k in range(3):
+            both_mats = []
+            for e in range(2):
+                mat = keep.tile([P, HALF + TWO_COUNT[k]], BF16, name="pool_mat%d%d" % (k, e))
+                first = TWO_COUNT[k] * e
+                pairs = half_ident[:].rearrange("p (j e) -> p j e", e=2)
+                nc.vector.tensor_tensor(
+                    out=mat[:, first : first + HALF], in0=pairs[:, :, 0], in1=pairs[:, :, 1], op=ADD
+                )
+                first = HALF * (1 - e)
+                for lo, hi in TWO_RUNS[k]:
+                    count = (hi - lo) // 4
+                    nc.vector.tensor_tensor(
+                        out=mat[:, first : first + count],
+                        in0=half_ident[:, lo:hi:4],
+                        in1=half_ident[:, lo + 2 : hi : 4],
+                        op=ADD,
+                    )
+                    first += count
+                both_mats.append(mat)
+            pool_mats.append(both_mats)
 
         ones = keep.tile([P, P], BF16)
         nc.vector.memset(ones[:], 1.0)
-        bias_row = keep.tile([P, KV], BF16)
-        nc.gpsimd.memset(bias_row[:], 0.0)
-        nc.vector.tensor_copy(out=bias_row[0:1, :], in_=bias_in[:])
         bias = keep.tile([P, KV], BF16)
 
         def spread_bias(r):
@@ -180,8 +183,12 @@ def tile_efficientmultiscaledilatedattention_pa_kernel(
             keep.tile([P, CH_PASSES, RANGE], U8, align_bytes=64, name="w_scales%d" % r)
             for r in range(RANGES)
         ]
-        xl_codes = keep.tile([P, LM_TILES, CH_PASSES, P], U32, align_bytes=64)
-        xl_scales = keep.tile([P, LM_TILES, CH_PASSES, P], U8, align_bytes=64)
+        xl_codes = keep.tile([P, GROUPS, CH_PASSES * K_PASS], U32, align_bytes=64)
+        xl_scales = keep.tile([P, GROUPS, CH_PASSES * K_PASS], U8, align_bytes=64)
+
+        def block(g, t, c):
+            i = PACK * c + t if g == GROUPS - 1 else CH_PASSES * t + c
+            return slice(P * i, P * (i + 1))
         e_codes = [
             keep.tile([P, GROUPS * COMPRESSED], U32, align_bytes=64, name="e_codes%d" % h)
             for h in range(2)
@@ -225,36 +232,62 @@ def tile_efficientmultiscaledilatedattention_pa_kernel(
             for lo, hi in ((0, 1024), (1024, 1152)):
                 quantise(nc, e_codes[h][:, lo:hi], e_scales[h][:, lo:hi], e_grouped[h][:, lo:hi, :])
 
-        xl_grouped = {}
+        xl_last = keep.tile([P, CH_PASSES * K_PASS, PACK], BF16, align_bytes=64)
+        xl_grouped = {GROUPS - 1: xl_last}
 
         def pool_landmarks(m, copy):
             g, t = m // PACK, m % PACK
-            if t == 0:
+            if t == 0 and g not in xl_grouped:
                 xl_grouped[g] = xl_stage.tile(
-                    [P, PACK, CH_PASSES, P, PACK], BF16, align_bytes=64, name="xl_grp"
+                    [P, CH_PASSES * K_PASS, PACK], BF16, align_bytes=64, name="xl_grp"
                 )
+            counts = [TWO_COUNT[(2 * m + e) % 3] for e in range(2)]
+            two_first = P + sum(TWO_COUNT[i % 3] for i in range(2 * m))
+            for c in range(CH_PASSES):
+                step = HALF + sum(counts)
+                mean = side_banks.tile([P, PACK, 2 * step], BF16, tag="side", name="side")
+                for s in range(PACK):
+                    chans = slice(K_PASS * c + P * s, K_PASS * c + P * (s + 1))
+                    for e in range(2):
+                        first = e * (HALF + counts[0])
+                        nc.tensor.matmul(
+                            out=mean[:, s, first : first + HALF + counts[e]],
+                            lhsT=token_tiles[2 * m + e][:, chans],
+                            rhs=pool_mats[(2 * m + e) % 3][e][:],
+                            start=True,
+                            stop=True,
+                        )
+                copy(
+                    out=xl_grouped[g][:, block(g, t, c), :].rearrange("p (e j) s -> p e j s", e=2),
+                    in_=mean[:].rearrange("p s (e x) -> p e x s", e=2)[:, :, 0:HALF, :],
+                )
+                first = K_PASS * c + two_first
+                copy(
+                    out=xl_last[:, first : first + sum(counts), :],
+                    in_=mean[:, :, HALF:step].rearrange("p s x -> p x s"),
+                )
+
+        def pool_three(copy):
             mean = side_banks.tile([P, CH_PASSES, PACK, P], BF16, tag="side", name="side")
             for c in range(CH_PASSES):
                 for s in range(PACK):
                     chans = slice(K_PASS * c + P * s, K_PASS * c + P * (s + 1))
-                    for e in range(2):
+                    for k in range(2):
                         nc.tensor.matmul(
-                            out=mean[:, c, s, HALF * e : HALF * (e + 1)],
-                            lhsT=token_tiles[2 * m + e][:, chans],
-                            rhs=(main_mat if m < MAIN_TILES else tail_mat)[:],
+                            out=mean[:, c, s, HALF * k : HALF * (k + 1)],
+                            lhsT=x_three[:, k, chans],
+                            rhs=pool_mats[0][0][:, 0:HALF],
                             start=True,
                             stop=True,
                         )
-            copy(out=xl_grouped[g][:, t, :, :, :], in_=mean[:].rearrange("p c s l -> p c l s"))
-
-        def quantise_landmarks(lo, hi):
-            g = lo // PACK
-            quantise(
-                nc,
-                xl_codes[:, lo:hi, :, :].rearrange("p m c l -> p (m c l)"),
-                xl_scales[:, lo:hi, :, :].rearrange("p m c l -> p (m c l)"),
-                xl_grouped[g][:, lo - PACK * g : hi - PACK * g, :, :, :].rearrange("p m c l s -> p (m c l) s"),
+            copy(
+                out=xl_last[:].rearrange("p (c l) s -> p c l s", c=CH_PASSES)[:, :, K_PASS - 96 :, :],
+                in_=mean[:, :, :, 0:96].rearrange("p c s l -> p c l s"),
             )
+
+        def quantise_landmarks(g, lo, hi):
+            part = slice(P * lo, P * hi)
+            quantise(nc, xl_codes[:, g, part], xl_scales[:, g, part], xl_grouped[g][:, part, :])
 
         acc = {}
         kv_codes = {}
@@ -266,12 +299,11 @@ def tile_efficientmultiscaledilatedattention_pa_kernel(
         def multiply(u, ct, t):
             r, g = UNITS[u]
             cols = slice(P * ct, P * (ct + 1))
-            m = PACK * g + t
             for c in range(CH_PASSES):
                 nc.tensor.matmul_mx(
                     out=acc[(u, ct)][:, t, :],
-                    lhsT=xl_codes[:, m, c, :].bitcast(FP8X4),
-                    lhsT_scale=xl_scales[:, m, c, :],
+                    lhsT=xl_codes[:, g, block(g, t, c)].bitcast(FP8X4),
+                    lhsT_scale=xl_scales[:, g, block(g, t, c)],
                     rhs=w_codes[r][:, c, cols].bitcast(FP8X4),
                     rhs_scale=w_scales[r][:, c, cols],
                     start=(c == 0),
@@ -351,25 +383,28 @@ def tile_efficientmultiscaledilatedattention_pa_kernel(
         def prep(a):
             k, i = a[0], int(a[1:])
             if k == "R":
-                spread_bias(i)
                 regroup_weights(i, [eng[z] for z in WENG[i]])
                 quantise_weights(i, i > 0)
             if k == "P":
                 pool_landmarks(i, eng[XENG[i]])
                 if i < 4:
-                    quantise_landmarks(i, i + 1)
-                elif i % XQ == XQ - 1:
-                    quantise_landmarks(i - XQ + 1, i + 1)
+                    quantise_landmarks(0, 2 * i, 2 * i + 2)
+                elif i < 8 and i % XQ == XQ - 1:
+                    quantise_landmarks(1, 2 * (i - 4 - XQ + 1), 2 * (i - 4) + 2)
+            if k == "T":
+                pool_three(eng[XENG[9]])
+                quantise_landmarks(2, 0, 8)
             if k == "E":
                 regroup_compressor(i)
                 quantise_compressor(i)
 
+        for r in range(RANGES):
+            spread_bias(r)
         for a in HEADP:
             prep(a)
         for ct in range(BANKS):
             open_bank(0, ct)
         for t in range(PACK):
-            prep("P%d" % t)
             for ct in range(BANKS):
                 multiply(0, ct, t)
         LAST = len(UNITS) - 1

@@ -38,7 +38,7 @@ WENG = ["vv", "vs", "vs", "ss"]
 XENG = "ssssssssssss"
 EENG = ["sss", "sss"]
 XQ = 2
-POS = {"R1": 0, "R2": 4, "P4": 4, "P5": 5, "P6": 6, "P7": 7, "P8": 12, "T0": 13, "E0": 26, "R3": 28, "E1": 34}
+POS = {"R1": 0, "R2": 4, "P4": 4, "P5": 5, "P6": 6, "P7": 7, "P8": 12, "T0": 13, "E0": 22, "R3": 28, "E1": 32}
 def two_runs(i):
     runs = []
     for row in range(0, GRID, 2):
@@ -356,6 +356,30 @@ def tile_efficientmultiscaledilatedattention_pa_kernel(
                 in_=result[:],
             )
 
+        def compress_last(r, ct):
+            h = r // 2
+            part = slice(P * ct, P * (ct + 1))
+            banks = [acc_banks.tile([P, PACK, P], F32, tag="acc", name="acc") for j in range(OUT_TILES)]
+            for g in range(GROUPS):
+                for j in range(OUT_TILES):
+                    rows = slice(COMPRESSED * g + P * j, COMPRESSED * g + P * (j + 1))
+                    nc.tensor.matmul_mx(
+                        out=banks[j][:, 0, :],
+                        lhsT=e_codes[h][:, rows].bitcast(FP8X4),
+                        lhsT_scale=e_scales[h][:, rows],
+                        rhs=kv_codes[r][:, g, part].bitcast(FP8X4),
+                        rhs_scale=kv_scales[r][:, g, part],
+                        start=(g == 0),
+                        stop=(g == GROUPS - 1),
+                    )
+            result = out_stage.tile([P, OUT_TILES, HEAD], F32, name="result")
+            for j in range(OUT_TILES):
+                copy = nc.scalar.copy if j == 1 else nc.vector.tensor_copy
+                copy(out=result[:, j, :], in_=banks[j][:, 0, :])
+                nc.sync.dma_start(
+                    out=outs[h][0, 4 * (r % 2) + ct, P * j : P * (j + 1), :], in_=result[:, j, :]
+                )
+
         def compress_wide(r, j):
             h = r // 2
             comp = side_banks.tile([P, RANGE], F32, tag="side", name="side")
@@ -428,7 +452,9 @@ def tile_efficientmultiscaledilatedattention_pa_kernel(
                 for r in range(RANGES):
                     last = max(i for i in range(12) if UNITS[i][0] == r)
                     if last == LAST:
-                        if u == LAST + 1:
+                        if u == LAST + 1 and ct < BANKS - 1:
                             compress(r, ct)
-                    elif u == last + 2 and ct > 0:
+                        elif u == LAST + 1:
+                            compress_last(r, ct)
+                    elif u == last + 1 and ct > 0:
                         compress_wide(r, ct - 1)

@@ -31,14 +31,14 @@ LM_TILES = LANDMARKS // P
 GRID = 48
 MAIN_TILES = 9
 
-LOADS = [("x", 0), ("x", 1), ("w", 0), ("x", 2), ("x", 3), ("w", 1), ("x", 4), ("x", 5), ("w", 2), ("x", 6), ("x", 7), ("e", 0), ("x", 8), ("t", 0), ("e", 1), ("w", 3)]
+LOADS = [("x", 0), ("w", 0), ("x", 1), ("x", 2), ("x", 3), ("w", 1), ("x", 4), ("x", 5), ("w", 2), ("x", 6), ("x", 7), ("e", 0), ("x", 8), ("t", 0), ("w", 3), ("e", 1)]
 MULT = mybir.AluOpType.mult
-HEADP = ["R0", "P0", "P1", "P2", "P3"]
-WENG = ["vv", "vs", "vs", "ss"]
-XENG = "ssssssssssss"
-EENG = ["sss", "sss"]
+HEADP = ["P0","R0","P1","P2","P3"]
+WENG = ["vv","vs","ss","ss"]
+XENG = "sssvssssssss"
+EENG = ["sss","sss"]
 XQ = 2
-POS = {"R1": 0, "R2": 4, "P4": 4, "P5": 5, "P6": 6, "P7": 7, "P8": 12, "T0": 13, "E0": 22, "R3": 28, "E1": 32}
+POS = {"R1": 0, "R2": 1, "P4": 0, "P5": 2, "P6": 4, "P7": 6, "P8": 18, "T0": 19, "E0": 22, "R3": 32, "E1": 32}
 def two_runs(i):
     runs = []
     for row in range(0, GRID, 2):

from contextlib import ExitStack

import concourse.mybir as mybir
from concourse.masks import make_identity

BF16 = mybir.dt.bfloat16
F32 = mybir.dt.float32
U32 = mybir.dt.uint32
U8 = mybir.dt.uint8
FP8X4 = mybir.dt.float8_e4m3fn_x4
ADD = mybir.AluOpType.add

P = 128
PACK = 4
K_PASS = P * PACK

CHANNELS = 1024
KV = 2048
LANDMARKS = 1536
COMPRESSED = 384
HEAD = 128

CH_PASSES = CHANNELS // K_PASS
GROUPS = LANDMARKS // K_PASS
RANGE = 512
RANGES = KV // RANGE
BANKS = RANGE // P
OUT_TILES = COMPRESSED // P
HALF = P // 2
LM_TILES = LANDMARKS // P
GRID = 48
MAIN_TILES = 9

LOADS = [("x", 0), ("w", 0), ("x", 1), ("x", 2), ("x", 3), ("w", 1), ("x", 4), ("x", 5), ("w", 2), ("x", 6), ("x", 7), ("e", 0), ("x", 8), ("t", 0), ("w", 3), ("e", 1)]
MULT = mybir.AluOpType.mult
HEADP = ["P0","R0","P1","P2","P3"]
WENG = ["vv","vs","ss","ss"]
XENG = "sssvssssssss"
EENG = ["sss","sss"]
XQ = 2
POS = {"R1": 0, "R2": 1, "P4": 0, "P5": 2, "P6": 4, "P7": 6, "P8": 18, "T0": 19, "E0": 22, "R3": 32, "E1": 32}
def two_runs(i):
    runs = []
    for row in range(0, GRID, 2):
        lo, hi = max(0, GRID * row - P * i), min(P, GRID * (row + 1) - P * i)
        if lo < hi:
            runs.append((lo, hi))
    return runs


TWO_RUNS = [two_runs(k) for k in range(3)]
TWO_COUNT = [sum(hi - lo for lo, hi in runs) // 4 for runs in TWO_RUNS]
UNITS = [(0, 0), (1, 0), (2, 0), (0, 1), (1, 1), (2, 1), (0, 2), (1, 2), (2, 2), (3, 0), (3, 1), (3, 2)]

FLOPS = 2 * LANDMARKS * CHANNELS * KV + 2 * 2 * COMPRESSED * LANDMARKS * CHANNELS


def regroup(copy, grouped, rows):
    copy(
        out=grouped.rearrange("p (c i) t -> p c t i", i=4),
        in_=rows.rearrange("p t (c i) -> p c t i", i=4),
    )


def quantise(nc, codes, scales, grouped):
    nc.vector.quantize_mx(
        out=codes.bitcast(FP8X4),
        scales=scales,
        in_=grouped.rearrange("p w t -> p (w t)"),
    )


def tile_efficientmultiscaledilatedattention_pa_kernel(
    tc, x, W_kv, b_kv, E_k, E_v, out_0, out_1
):
    nc = tc.nc
    with ExitStack() as ctx:
        keep = ctx.enter_context(tc.tile_pool(name="keep", bufs=1))
        w_stage = ctx.enter_context(tc.tile_pool(name="w_stage", bufs=2))
        e_stage = ctx.enter_context(tc.tile_pool(name="e_stage", bufs=1))
        xl_stage = ctx.enter_context(tc.tile_pool(name="xl_stage", bufs=2))
        kv_stage = ctx.enter_context(tc.tile_pool(name="kv_stage", bufs=2))
        kv_keep = ctx.enter_context(tc.tile_pool(name="kv_keep", bufs=3))
        out_stage = ctx.enter_context(tc.tile_pool(name="out_stage", bufs=4))
        acc_banks = ctx.enter_context(tc.psum_pool(name="acc_banks", bufs=BANKS))
        side_banks = ctx.enter_context(tc.psum_pool(name="side_banks", bufs=4))

        bias_in = keep.tile([1, KV], BF16)
        nc.sync.dma_start(out=bias_in[:], in_=b_kv.unsqueeze(0))
        bias_row = keep.tile([P, KV], BF16)
        nc.vector.memset(bias_row[:], 0.0)
        nc.vector.tensor_copy(out=bias_row[0:1, :], in_=bias_in[:])

        w_view = W_kv.rearrange("(s p) n -> p s n", p=P)
        w_raw = [
            keep.tile([P, CH_PASSES * PACK, RANGE], BF16, name="w_raw%d" % r) for r in range(RANGES)
        ]

        def load_weights(r):
            for c in range(CH_PASSES):
                slots = slice(PACK * c, PACK * (c + 1))
                nc.sync.dma_start(
                    out=w_raw[r][:, slots, :], in_=w_view[:, slots, RANGE * r : RANGE * (r + 1)]
                )

        tokens = x.flatten_outer_dims()
        token_tiles = []

        def load_main(m):
            x_main = keep.tile([P, 2, CHANNELS], BF16, name="x_main%d" % m)
            nc.sync.dma_start(
                out=x_main[:],
                in_=tokens[2 * P * m : 2 * P * (m + 1), :].rearrange("(e p) c -> p e c", p=P),
            )
            token_tiles.extend([x_main[:, 0, :], x_main[:, 1, :]])

        x_three = keep.tile([P, 2, CHANNELS], BF16)

        def load_tail():
            by_three = tokens.rearrange("(k b r c e) d -> b r e c k d", k=2, b=8, r=3, c=16, e=3)
            for b in range(8):
                nc.sync.dma_start(out=x_three[16 * b : 16 * (b + 1), :, :], in_=by_three[b, 0, 0])

        e_raw = [
            keep.tile([P, LM_TILES, COMPRESSED], BF16, name="e_raw%d" % h) for h in range(2)
        ]

        def load_compressor(h):
            nc.sync.dma_start(out=e_raw[h][:], in_=(E_k, E_v)[h].rearrange("(s p) j -> p s j", p=P))

        for what, i in LOADS:
            if what == "w":
                load_weights(i)
            if what == "x":
                load_main(i)
            if what == "t":
                load_tail()
            if what == "e":
                load_compressor(i)

        ident = keep.tile([P, P], BF16)
        make_identity(nc, ident[:])
        half_ident = keep.tile([P, P], BF16)
        nc.vector.tensor_scalar_mul(out=half_ident[:], in0=ident[:], scalar1=0.5)
        pool_mats = []
        for k in range(3):
            both_mats = []
            for e in range(2):
                mat = keep.tile([P, HALF + TWO_COUNT[k]], BF16, name="pool_mat%d%d" % (k, e))
                first = TWO_COUNT[k] * e
                pairs = half_ident[:].rearrange("p (j e) -> p j e", e=2)
                nc.vector.tensor_tensor(
                    out=mat[:, first : first + HALF], in0=pairs[:, :, 0], in1=pairs[:, :, 1], op=ADD
                )
                first = HALF * (1 - e)
                for lo, hi in TWO_RUNS[k]:
                    count = (hi - lo) // 4
                    nc.vector.tensor_tensor(
                        out=mat[:, first : first + count],
                        in0=half_ident[:, lo:hi:4],
                        in1=half_ident[:, lo + 2 : hi : 4],
                        op=ADD,
                    )
                    first += count
                both_mats.append(mat)
            pool_mats.append(both_mats)

        ones = keep.tile([P, P], BF16)
        nc.vector.memset(ones[:], 1.0)
        bias = keep.tile([P, KV], BF16)

        def spread_bias(r):
            cols = slice(RANGE * r, RANGE * (r + 1))
            spread = side_banks.tile([P, RANGE], F32, tag="side", name="side")
            nc.tensor.matmul(out=spread[:], lhsT=ones[:], rhs=bias_row[:, cols], start=True, stop=True)
            nc.scalar.copy(out=bias[:, cols], in_=spread[:])

        w_codes = [
            keep.tile([P, CH_PASSES, RANGE], U32, align_bytes=64, name="w_codes%d" % r)
            for r in range(RANGES)
        ]
        w_scales = [
            keep.tile([P, CH_PASSES, RANGE], U8, align_bytes=64, name="w_scales%d" % r)
            for r in range(RANGES)
        ]
        xl_codes = keep.tile([P, GROUPS, CH_PASSES * K_PASS], U32, align_bytes=64)
        xl_scales = keep.tile([P, GROUPS, CH_PASSES * K_PASS], U8, align_bytes=64)

        def block(g, t, c):
            i = PACK * c + t if g == GROUPS - 1 else CH_PASSES * t + c
            return slice(P * i, P * (i + 1))
        e_codes = [
            keep.tile([P, GROUPS * COMPRESSED], U32, align_bytes=64, name="e_codes%d" % h)
            for h in range(2)
        ]
        e_scales = [
            keep.tile([P, GROUPS * COMPRESSED], U8, align_bytes=64, name="e_scales%d" % h)
            for h in range(2)
        ]

        w_grouped = {}

        def regroup_weights(r, copies):
            w_grouped[r] = w_stage.tile([P, CH_PASSES, RANGE, PACK], BF16, align_bytes=64, name="w_grp")
            for c in range(CH_PASSES):
                regroup(copies[c], w_grouped[r][:, c, :, :], w_raw[r][:, PACK * c : PACK * (c + 1), :])

        def quantise_weights(r, whole):
            if whole:
                quantise(
                    nc,
                    w_codes[r][:].rearrange("p c n -> p (c n)"),
                    w_scales[r][:].rearrange("p c n -> p (c n)"),
                    w_grouped[r][:].rearrange("p c n t -> p (c n) t"),
                )
            else:
                for c in range(CH_PASSES):
                    quantise(nc, w_codes[r][:, c, :], w_scales[r][:, c, :], w_grouped[r][:, c, :, :])

        e_grouped = {}

        def regroup_compressor(h):
            e_grouped[h] = e_stage.tile([P, GROUPS * COMPRESSED, PACK], BF16, align_bytes=64, name="e_grp")
            for g in range(GROUPS):
                regroup(
                    eng[EENG[h][g]],
                    e_grouped[h][:, COMPRESSED * g : COMPRESSED * (g + 1), :],
                    e_raw[h][:, PACK * g : PACK * (g + 1), :],
                )

        def quantise_compressor(h):
            for lo, hi in ((0, 1024), (1024, 1152)):
                quantise(nc, e_codes[h][:, lo:hi], e_scales[h][:, lo:hi], e_grouped[h][:, lo:hi, :])

        xl_last = keep.tile([P, CH_PASSES * K_PASS, PACK], BF16, align_bytes=64)
        xl_grouped = {GROUPS - 1: xl_last}

        def pool_landmarks(m, copy):
            g, t = m // PACK, m % PACK
            if t == 0 and g not in xl_grouped:
                xl_grouped[g] = xl_stage.tile(
                    [P, CH_PASSES * K_PASS, PACK], BF16, align_bytes=64, name="xl_grp"
                )
            counts = [TWO_COUNT[(2 * m + e) % 3] for e in range(2)]
            two_first = P + sum(TWO_COUNT[i % 3] for i in range(2 * m))
            for c in range(CH_PASSES):
                step = HALF + sum(counts)
                mean = side_banks.tile([P, PACK, 2 * step], BF16, tag="side", name="side")
                for s in range(PACK):
                    chans = slice(K_PASS * c + P * s, K_PASS * c + P * (s + 1))
                    for e in range(2):
                        first = e * (HALF + counts[0])
                        nc.tensor.matmul(
                            out=mean[:, s, first : first + HALF + counts[e]],
                            lhsT=token_tiles[2 * m + e][:, chans],
                            rhs=pool_mats[(2 * m + e) % 3][e][:],
                            start=True,
                            stop=True,
                        )
                copy(
                    out=xl_grouped[g][:, block(g, t, c), :].rearrange("p (e j) s -> p e j s", e=2),
                    in_=mean[:].rearrange("p s (e x) -> p e x s", e=2)[:, :, 0:HALF, :],
                )
                first = K_PASS * c + two_first
                copy(
                    out=xl_last[:, first : first + sum(counts), :],
                    in_=mean[:, :, HALF:step].rearrange("p s x -> p x s"),
                )

        def pool_three(copy):
            mean = side_banks.tile([P, CH_PASSES, PACK, P], BF16, tag="side", name="side")
            for c in range(CH_PASSES):
                for s in range(PACK):
                    chans = slice(K_PASS * c + P * s, K_PASS * c + P * (s + 1))
                    for k in range(2):
                        nc.tensor.matmul(
                            out=mean[:, c, s, HALF * k : HALF * (k + 1)],
                            lhsT=x_three[:, k, chans],
                            rhs=pool_mats[0][0][:, 0:HALF],
                            start=True,
                            stop=True,
                        )
            copy(
                out=xl_last[:].rearrange("p (c l) s -> p c l s", c=CH_PASSES)[:, :, K_PASS - 96 :, :],
                in_=mean[:, :, :, 0:96].rearrange("p c s l -> p c l s"),
            )

        def quantise_landmarks(g, lo, hi):
            part = slice(P * lo, P * hi)
            quantise(nc, xl_codes[:, g, part], xl_scales[:, g, part], xl_grouped[g][:, part, :])

        acc = {}
        kv_codes = {}
        kv_scales = {}

        def open_bank(u, ct):
            acc[(u, ct)] = acc_banks.tile([P, PACK, P], F32, tag="acc", name="acc")

        def multiply(u, ct, t):
            r, g = UNITS[u]
            cols = slice(P * ct, P * (ct + 1))
            for c in range(CH_PASSES):
                nc.tensor.matmul_mx(
                    out=acc[(u, ct)][:, t, :],
                    lhsT=xl_codes[:, g, block(g, t, c)].bitcast(FP8X4),
                    lhsT_scale=xl_scales[:, g, block(g, t, c)],
                    rhs=w_codes[r][:, c, cols].bitcast(FP8X4),
                    rhs_scale=w_scales[r][:, c, cols],
                    start=(c == 0),
                    stop=(c == CH_PASSES - 1),
                )

        kv_grouped = {}

        def drain(u, ct):
            r, g = UNITS[u]
            if ct == 0:
                kv_grouped[u] = kv_stage.tile([P, RANGE, PACK], BF16, align_bytes=64, name="kv_grp")
            cols = slice(RANGE * r + P * ct, RANGE * r + P * (ct + 1))
            nc.vector.tensor_tensor(
                out=kv_grouped[u][:, P * ct : P * (ct + 1), :],
                in0=acc[(u, ct)][:].rearrange("p t n -> p n t"),
                in1=bias[:, cols].unsqueeze(2).to_broadcast([P, P, PACK]),
                op=ADD,
            )

        def quantise_unit(u, lo, hi):
            r, g = UNITS[u]
            if r not in kv_codes:
                kv_codes[r] = kv_keep.tile([P, GROUPS, RANGE], U32, align_bytes=64, name="kv_codes")
                kv_scales[r] = kv_keep.tile([P, GROUPS, RANGE], U8, align_bytes=64, name="kv_scales")
            quantise(nc, kv_codes[r][:, g, lo:hi], kv_scales[r][:, g, lo:hi], kv_grouped[u][:, lo:hi, :])

        outs = [out_0, out_1]

        def compress(r, ct):
            h = r // 2
            part = slice(P * ct, P * (ct + 1))
            comp = side_banks.tile([P, OUT_TILES, HEAD], F32, tag="side", name="side")
            for j in range(OUT_TILES):
                for g in range(GROUPS):
                    rows = slice(COMPRESSED * g + P * j, COMPRESSED * g + P * (j + 1))
                    nc.tensor.matmul_mx(
                        out=comp[:, j, :],
                        lhsT=e_codes[h][:, rows].bitcast(FP8X4),
                        lhsT_scale=e_scales[h][:, rows],
                        rhs=kv_codes[r][:, g, part].bitcast(FP8X4),
                        rhs_scale=kv_scales[r][:, g, part],
                        start=(g == 0),
                        stop=(g == GROUPS - 1),
                    )
            result = out_stage.tile([P, OUT_TILES, HEAD], F32, name="result")
            nc.scalar.copy(out=result[:], in_=comp[:])
            nc.sync.dma_start(
                out=outs[h][0, 4 * (r % 2) + ct, :, :].rearrange("(j p) d -> p j d", p=P),
                in_=result[:],
            )

        def compress_last(r, ct):
            h = r // 2
            part = slice(P * ct, P * (ct + 1))
            banks = [acc_banks.tile([P, PACK, P], F32, tag="acc", name="acc") for j in range(OUT_TILES)]
            for g in range(GROUPS):
                for j in range(OUT_TILES):
                    rows = slice(COMPRESSED * g + P * j, COMPRESSED * g + P * (j + 1))
                    nc.tensor.matmul_mx(
                        out=banks[j][:, 0, :],
                        lhsT=e_codes[h][:, rows].bitcast(FP8X4),
                        lhsT_scale=e_scales[h][:, rows],
                        rhs=kv_codes[r][:, g, part].bitcast(FP8X4),
                        rhs_scale=kv_scales[r][:, g, part],
                        start=(g == 0),
                        stop=(g == GROUPS - 1),
                    )
            result = out_stage.tile([P, OUT_TILES, HEAD], F32, name="result")
            for j in range(OUT_TILES):
                copy = nc.scalar.copy if j == 1 else nc.vector.tensor_copy
                copy(out=result[:, j, :], in_=banks[j][:, 0, :])
                nc.sync.dma_start(
                    out=outs[h][0, 4 * (r % 2) + ct, P * j : P * (j + 1), :], in_=result[:, j, :]
                )

        def compress_wide(r, j):
            h = r // 2
            comp = side_banks.tile([P, RANGE], F32, tag="side", name="side")
            for g in range(GROUPS):
                rows = slice(COMPRESSED * g + P * j, COMPRESSED * g + P * (j + 1))
                nc.tensor.matmul_mx(
                    out=comp[:],
                    lhsT=e_codes[h][:, rows].bitcast(FP8X4),
                    lhsT_scale=e_scales[h][:, rows],
                    rhs=kv_codes[r][:, g, :].bitcast(FP8X4),
                    rhs_scale=kv_scales[r][:, g, :],
                    start=(g == 0),
                    stop=(g == GROUPS - 1),
                )
            result = out_stage.tile([P, RANGE], F32, name="result")
            nc.scalar.copy(out=result[:], in_=comp[:])
            heads = slice(4 * (r % 2), 4 * (r % 2) + 4)
            nc.sync.dma_start(
                out=outs[h][0, heads, P * j : P * (j + 1), :].rearrange("h j d -> j h d"),
                in_=result[:].rearrange("p (h d) -> p h d", d=HEAD),
            )

        eng = {"v": nc.vector.tensor_copy, "s": nc.scalar.copy, "g": lambda out, in_: nc.gpsimd.tensor_scalar(out=out, in0=in_, scalar1=1.0, scalar2=0.0, op0=MULT, op1=ADD)}

        def prep(a):
            k, i = a[0], int(a[1:])
            if k == "R":
                regroup_weights(i, [eng[z] for z in WENG[i]])
                quantise_weights(i, i > 0)
            if k == "P":
                pool_landmarks(i, eng[XENG[i]])
                if i < 4:
                    quantise_landmarks(0, 2 * i, 2 * i + 2)
                elif i < 8 and i % XQ == XQ - 1:
                    quantise_landmarks(1, 2 * (i - 4 - XQ + 1), 2 * (i - 4) + 2)
            if k == "T":
                pool_three(eng[XENG[9]])
                quantise_landmarks(2, 0, 8)
            if k == "E":
                regroup_compressor(i)
                quantise_compressor(i)

        for r in range(RANGES):
            spread_bias(r)
        for a in HEADP:
            prep(a)
        for ct in range(BANKS):
            open_bank(0, ct)
        for t in range(PACK):
            for ct in range(BANKS):
                multiply(0, ct, t)
        LAST = len(UNITS) - 1
        for u in range(len(UNITS) + 2):
            for ct in range(BANKS):
                for a, pos in POS.items():
                    if pos == 4 * u + ct:
                        prep(a)
                if u <= LAST:
                    drain(u, ct)
                if ct == 0 and 0 < u <= LAST:
                    quantise_unit(u - 1, 0, RANGE)
                if u == LAST and ct > 0:
                    quantise_unit(u, P * (ct - 1), P * ct)
                if u == LAST + 1 and ct == 0:
                    quantise_unit(LAST, RANGE - P, RANGE)
                if u + 1 <= LAST:
                    open_bank(u + 1, ct)
                    for t in range(PACK):
                        multiply(u + 1, ct, t)
                for r in range(RANGES):
                    last = max(i for i in range(12) if UNITS[i][0] == r)
                    if last == LAST:
                        if u == LAST + 1 and ct < BANKS - 1:
                            compress(r, ct)
                        elif u == LAST + 1:
                            compress_last(r, ct)
                    elif u == last + 1 and ct > 0:
                        compress_wide(r, ct - 1)
